import numpy as np
import ml_dtypes


def mxq(x, axis, fmt="e4m3"):
    dtype, down = {"e4m3": (ml_dtypes.float8_e4m3fn, 7), "e5m2": (ml_dtypes.float8_e5m2, 14)}[fmt]
    v = np.moveaxis(np.asarray(x, np.float32).astype(ml_dtypes.bfloat16).astype(np.float64), axis, -1)
    blocks = v.reshape(v.shape[:-1] + (-1, 32))
    amax = np.abs(blocks).max(-1, keepdims=True)
    byte = np.maximum(np.where(amax > 0, np.frexp(amax)[1] - 1 + 127, 0) - down, 1)
    scale = np.exp2(byte - 127.0)
    codes = (blocks / scale).astype(np.float32).astype(dtype).astype(np.float64)
    return np.moveaxis((codes * scale).reshape(v.shape), -1, axis)


WIDE = False


def mx_kscale(k):
    if not WIDE:
        return np.ones(k)
    levels = np.array([10, -10, 5, -5, 0])
    a = np.random.permutation(np.resize(levels, k // 512 * 4)).reshape(k // 512, 4)
    idx = np.arange(k)
    return np.exp2(a[idx // 512, idx % 128 // 32])


BF16 = ml_dtypes.bfloat16


def bf(x):
    return np.asarray(x, np.float32).astype(BF16)


def f64(x):
    return np.asarray(x).astype(np.float64)


E2M1 = np.array([0.0, 0.5, 1.0, 1.5, 2.0, 3.0, 4.0, 6.0, -0.0, -0.5, -1.0, -1.5, -2.0, -3.0, -4.0, -6.0])


def pack_weight(w, fmt):
    k, n = w.shape
    w = f64(bf(w)).reshape(k // 32, 32, n)
    amax = np.abs(w).max(1)
    if fmt == "e4m3":
        byte = np.frexp(amax)[1] - 1 + 127 - 7
    else:
        mant, ex = np.frexp(amax / 6.0)
        byte = np.where(mant > 0.5, ex, ex - 1) + 127
    byte = np.clip(np.where(amax > 0, byte, 1), 1, 254)
    scaled = (w * np.exp2(127.0 - byte)[:, None, :]).reshape(k, n).astype(np.float32)
    by_word = np.ascontiguousarray(scaled.reshape(k // 512, 128, 4, n).transpose(0, 1, 3, 2))
    if fmt == "e4m3":
        words = by_word.astype(ml_dtypes.float8_e4m3fn).view(np.uint8)
    else:
        c = by_word.astype(ml_dtypes.float4_e2m1fn).view(np.uint8) & 0xF
        words = c[..., 0::2] | (c[..., 1::2] << 4)
    return np.ascontiguousarray(words), np.ascontiguousarray(byte.astype(np.uint8).reshape(k // 512, 16, n))


def unpack_weight(words, scales, fmt):
    g, p, n, _ = words.shape
    if fmt == "e4m3":
        vals = np.ascontiguousarray(words).view(ml_dtypes.float8_e4m3fn).astype(np.float64)
    else:
        nib = np.empty((g, p, n, 4), np.uint8)
        nib[..., 0::2] = words & 0xF
        nib[..., 1::2] = words >> 4
        vals = E2M1[nib]
    vals = vals * np.repeat(np.exp2(scales.astype(np.float64) - 127.0), 8, axis=1)[..., None]
    return vals.transpose(0, 1, 3, 2).reshape(g * 512, n)


B, C, CO, H, W = 2, 2048, 512, 24, 24
EPS = 1e-5
POOL_SIZES = (1, 2, 3, 6)
N = H * W
FMT = "e4m3"


def bn_relu(y, scale, bias, mean, var):
    inv = scale / np.sqrt(var + EPS)
    return np.maximum((y - mean[None, :, None]) * inv[None, :, None] + bias[None, :, None], 0.0)


def pyramid_pool(f):
    feats = []
    for s in POOL_SIZES:
        p = f.reshape(B, CO, s, H // s, s, W // s).mean(axis=(3, 5))
        feats.append(p.reshape(B, CO, s * s))
    return np.concatenate(feats, axis=-1)


def setup_inputs():
    s = mx_kscale(C)
    d = {}
    d["x"] = bf(np.random.standard_normal((B, C, H, W)) * s[None, :, None, None])
    for n in ("q", "k"):
        w = np.random.standard_normal((CO, C)) * 0.5 / np.sqrt(C) / s[None, :]
        words, scales = pack_weight(np.ascontiguousarray(w.T), FMT)
        d["w" + n + "_words"] = words
        d["w" + n + "_scales"] = scales
        d[n + "_scale"] = bf(np.random.uniform(0.5, 1.5, CO))
        d[n + "_bias"] = bf(np.random.standard_normal(CO) * 0.1)
        d[n + "_mean"] = bf(np.random.standard_normal(CO) * 0.1)
        d[n + "_var"] = bf(np.random.uniform(0.5, 1.5, CO))
    return d


def reference(x, wq_words, wq_scales, q_scale, q_bias, q_mean, q_var, wk_words, wk_scales, k_scale, k_bias, k_mean, k_var):
    xq = mxq(f64(x).reshape(B, C, N), 1, "e4m3")
    yq = unpack_weight(wq_words, wq_scales, FMT).T @ xq
    yk = unpack_weight(wk_words, wk_scales, FMT).T @ xq
    q = pyramid_pool(bn_relu(yq, f64(q_scale), f64(q_bias), f64(q_mean), f64(q_var)))
    k = pyramid_pool(bn_relu(yk, f64(k_scale), f64(k_bias), f64(k_mean), f64(k_var)))
    return q, k

@@ -1,0 +1,273 @@
+from contextlib import ExitStack
+
+import concourse.mybir as mybir
+from concourse.masks import make_identity
+
+BF16 = mybir.dt.bfloat16
+F32 = mybir.dt.float32
+I32 = mybir.dt.int32
+U32 = mybir.dt.uint32
+U8 = mybir.dt.uint8
+FP8X4 = mybir.dt.float8_e4m3fn_x4
+ADD = mybir.AluOpType.add
+RELU = mybir.ActivationFunctionType.Relu
+
+P = 128
+PACK = 4
+K_PASS = P * PACK
+BATCH = 2
+CHANNELS = 2048
+GROUPS = CHANNELS // K_PASS
+CO = 512
+BRANCHES = 2
+CO_TILES = CO // P
+M_TILES = BRANCHES * CO_TILES
+SIDE = 24
+POS = SIDE * SIDE
+COLS = BATCH * POS
+CELL = 4
+GRID = SIDE // CELL
+BAND = CELL * SIDE
+BANDS = COLS // BAND
+EPS = 1e-5
+FEATS = 50
+
+FIRST = (0, 512)
+MIDDLE = (512, 640)
+LAST = (640, 1152)
+
+VECTOR_COLS = 384
+
+FLOPS = 2 * BRANCHES * BATCH * CO * CHANNELS * POS
+
+
+def tile_guided_cam_module2_pa_kernel(
+    tc,
+    x,
+    wq_words,
+    wq_scales,
+    q_scale,
+    q_bias,
+    q_mean,
+    q_var,
+    wk_words,
+    wk_scales,
+    k_scale,
+    k_bias,
+    k_mean,
+    k_var,
+    out_0,
+    out_1,
+):
+    nc = tc.nc
+    words_in = (wq_words, wk_words)
+    scales_in = (wq_scales, wk_scales)
+    bn_in = (q_scale, q_bias, q_mean, q_var, k_scale, k_bias, k_mean, k_var)
+    outs = (out_0, out_1)
+    x_rows = x.rearrange("b c h w -> b c (h w)")
+
+    with ExitStack() as stack:
+        keep = stack.enter_context(tc.tile_pool(name="keep", bufs=1))
+        stage = stack.enter_context(tc.tile_pool(name="stage", bufs=4))
+        psum = stack.enter_context(tc.psum_pool(name="psum", bufs=8))
+
+        raw = [
+            [keep.tile([P, PACK, POS], BF16, name="raw%d%d" % (b, g)) for g in range(GROUPS)]
+            for b in range(BATCH)
+        ]
+        w_words = [
+            keep.tile([P, GROUPS, CO], U32, name="w_words%d" % br, align_bytes=64)
+            for br in range(BRANCHES)
+        ]
+        w_planes = keep.tile([P, BRANCHES, CO], U8, name="w_planes", align_bytes=64)
+        x_words = keep.tile([P, GROUPS, COLS], U32, name="x_words", align_bytes=64)
+        x_planes = keep.tile([P, GROUPS, COLS], U8, name="x_planes", align_bytes=64)
+        bn_rows = keep.tile([P, P], BF16, name="bn_rows")
+        ident = keep.tile([P, P], BF16, name="ident")
+        z = keep.tile([P, M_TILES, COLS], F32, name="z")
+        cell_sums = keep.tile([P, M_TILES, BANDS * GRID], F32, name="cell_sums")
+
+        nc.vector.memset(w_planes[:].bitcast(I32), 0)
+        nc.vector.memset(bn_rows[:], 0.0)
+        make_identity(nc, ident[:])
+
+        def load_x(b, g):
+            rows = x_rows[b, g * K_PASS : (g + 1) * K_PASS, :]
+            nc.sync.dma_start(out=raw[b][g][:], in_=rows.rearrange("(p t) n -> p t n", t=PACK))
+
+        def load_words(g):
+            for br in range(BRANCHES):
+                nc.sync.dma_start(
+                    out=w_words[br][:, g, :].bitcast(I32),
+                    in_=words_in[br][g].rearrange("p n t -> p (n t)").bitcast(I32),
+                )
+
+        load_x(0, 0)
+        load_words(0)
+        for br in range(BRANCHES):
+            for quad in range(4):
+                nc.sync.dma_start(
+                    out=w_planes[32 * quad : 32 * quad + 16, br, :].bitcast(I32),
+                    in_=scales_in[br][:, 4 * quad : 4 * quad + 4, :].bitcast(I32),
+                )
+        load_x(0, 1)
+        load_words(1)
+        for v in range(len(bn_in)):
+            nc.scalar.dma_start(
+                out=bn_rows[CO_TILES * v : CO_TILES * (v + 1), :],
+                in_=bn_in[v].rearrange("(c p) -> c p", p=P),
+            )
+        for g in range(2, GROUPS):
+            load_x(0, g)
+            load_words(g)
+        for g in range(GROUPS):
+            load_x(1, g)
+
+        bn_ps = psum.tile([P, P], BF16, tag="acc")
+        nc.tensor.transpose(bn_ps[:], bn_rows[:], ident[:])
+        bn = keep.tile([P, BRANCHES, 4, CO_TILES], F32, name="bn")
+        nc.vector.tensor_copy(
+            out=bn[:].rearrange("p b k c -> p (b k c)"), in_=bn_ps[:, 0 : BRANCHES * 4 * CO_TILES]
+        )
+        gain, bias, mean, var = [bn[:, :, kind, :] for kind in range(4)]
+        rstd = keep.tile([P, BRANCHES, CO_TILES], F32, name="rstd")
+        slope = keep.tile([P, BRANCHES, CO_TILES], F32, name="slope")
+        shift = keep.tile([P, BRANCHES, CO_TILES], F32, name="shift")
+        nc.vector.tensor_scalar_add(out=rstd[:], in0=var, scalar1=EPS)
+        nc.scalar.sqrt(out=rstd[:], in_=rstd[:])
+        nc.vector.reciprocal(out=rstd[:], in_=rstd[:])
+        nc.vector.tensor_mul(out=slope[:], in0=gain, in1=rstd[:])
+        nc.vector.tensor_mul(out=shift[:], in0=mean, in1=slope[:])
+        nc.vector.tensor_sub(out=shift[:], in0=bias, in1=shift[:])
+        slope_m = slope[:].rearrange("p b c -> p (b c)")
+        shift_m = shift[:].rearrange("p b c -> p (b c)")
+
+        def quantise_slab(b, g):
+            grouped = stage.tile([P, POS, PACK], BF16, tag="grouped", align_bytes=64)
+            nc.vector.tensor_copy(
+                out=grouped[:, 0:VECTOR_COLS, :].rearrange("p (c i) t -> p c t i", i=4),
+                in_=raw[b][g][:, :, 0:VECTOR_COLS].rearrange("p t (c i) -> p c t i", i=4),
+            )
+            nc.scalar.copy(
+                out=grouped[:, VECTOR_COLS:POS, :].rearrange("p (c i) t -> p c t i", i=4),
+                in_=raw[b][g][:, :, VECTOR_COLS:POS].rearrange("p t (c i) -> p c t i", i=4),
+            )
+            cut = 512 if b == 0 else 64
+            for lo, hi in ((0, cut), (cut, POS)):
+                nc.vector.quantize_mx(
+                    out=x_words[:, g, b * POS + lo : b * POS + hi].bitcast(FP8X4),
+                    scales=x_planes[:, g, b * POS + lo : b * POS + hi],
+                    in_=grouped[:, lo:hi, :].rearrange("p n t -> p (n t)"),
+                )
+
+        def mx_pass(acc, m, g, cols):
+            br, co = divmod(m, CO_TILES)
+            co_cols = slice(co * P, (co + 1) * P)
+            nc.tensor.matmul_mx(
+                out=acc,
+                lhsT=w_words[br][:, g, co_cols].bitcast(FP8X4),
+                lhsT_scale=w_planes[4 * g : P, br, co_cols],
+                rhs=x_words[:, g, cols[0] : cols[1]].bitcast(FP8X4),
+                rhs_scale=x_planes[:, g, cols[0] : cols[1]],
+                start=(g == 0),
+                stop=(g == GROUPS - 1),
+            )
+
+        def new_acc(cols):
+            acc = psum.tile([P, 512], F32, tag="acc")
+            return acc[:, 0 : cols[1] - cols[0]]
+
+        def bn_relu(acc, m, cols):
+            nc.scalar.activation(
+                out=z[:, m, cols[0] : cols[1]],
+                in_=acc,
+                func=RELU,
+                bias=shift_m[:, m : m + 1],
+                scale=slope_m[:, m : m + 1],
+            )
+
+        def pool_bands(m, first, stop):
+            nc.vector.tensor_reduce(
+                out=cell_sums[:, m, first * GRID : stop * GRID].rearrange(
+                    "p (r c) -> p r c", c=GRID
+                ),
+                in_=z[:, m, first * BAND : stop * BAND].rearrange(
+                    "p (r i c j) -> p r c i j", i=CELL, c=GRID, j=CELL
+                ),
+                axis=mybir.AxisListType.XY,
+                op=ADD,
+            )
+
+        def finish_branch(br):
+            sums = cell_sums[:, br * CO_TILES : (br + 1) * CO_TILES, :]
+            res = keep.tile([P, BATCH, CO_TILES, FEATS], F32, name="res%d" % br)
+            sums3 = keep.tile([P, CO_TILES, BATCH, 9], F32, name="sums3_%d" % br)
+            sums2 = keep.tile([P, CO_TILES, BATCH, 4], F32, name="sums2_%d" % br)
+            sums1 = keep.tile([P, CO_TILES, BATCH, 1], F32, name="sums1_%d" % br)
+            nc.vector.tensor_reduce(
+                out=sums3[:].rearrange("p m b (r c) -> p (m b r) c", c=3),
+                in_=sums.rearrange("p m (b r i c j) -> p (m b r) c i j", b=BATCH, r=3, i=2, c=3, j=2),
+                axis=mybir.AxisListType.XY,
+                op=ADD,
+            )
+            nc.vector.tensor_reduce(
+                out=sums2[:].rearrange("p m b (r c) -> p (m b r) c", c=2),
+                in_=sums.rearrange("p m (b r i c j) -> p (m b r) c i j", b=BATCH, r=2, i=3, c=2, j=3),
+                axis=mybir.AxisListType.XY,
+                op=ADD,
+            )
+            nc.vector.tensor_reduce(
+                out=sums1[:].rearrange("p m b o -> p (m b) o"),
+                in_=sums2[:].rearrange("p m b f -> p (m b) f"),
+                axis=mybir.AxisListType.X,
+                op=ADD,
+            )
+            for level_sums, first, side in (
+                (sums1[:], 0, 1),
+                (sums2[:], 1, 2),
+                (sums3[:], 5, 3),
+                (sums.rearrange("p m (b f) -> p m b f", b=BATCH), 14, 6),
+            ):
+                nc.vector.tensor_scalar_mul(
+                    out=res[:, :, :, first : first + side * side].rearrange("p b m f -> p m b f"),
+                    in0=level_sums,
+                    scalar1=float(side * side) / POS,
+                )
+            nc.sync.dma_start(
+                out=outs[br].rearrange("b (m p) f -> p (b m) f", p=P),
+                in_=res[:].rearrange("p b m f -> p (b m) f"),
+            )
+
+        accs = [new_acc(FIRST) for m in range(M_TILES)]
+        for g in range(GROUPS):
+            quantise_slab(0, g)
+            for m in range(M_TILES):
+                mx_pass(accs[m], m, g, FIRST)
+        for g in range(GROUPS):
+            quantise_slab(1, g)
+        for m in range(M_TILES):
+            bn_relu(accs[m], m, FIRST)
+            pool_bands(m, 0, 5)
+
+        accs = [new_acc(LAST) for m in range(CO_TILES)]
+        for g in range(GROUPS):
+            for m in range(CO_TILES):
+                mx_pass(accs[m], m, g, LAST)
+        for m in range(CO_TILES):
+            bn_relu(accs[m], m, LAST)
+            pool_bands(m, 7, 12)
+        for m in range(CO_TILES, M_TILES):
+            acc = new_acc(LAST)
+            for g in range(GROUPS):
+                mx_pass(acc, m, g, LAST)
+            bn_relu(acc, m, LAST)
+            pool_bands(m, 7, 12)
+
+        for m in range(M_TILES):
+            acc = new_acc(MIDDLE)
+            for g in range(GROUPS):
+                mx_pass(acc, m, g, MIDDLE)
+            bn_relu(acc, m, MIDDLE)
+            pool_bands(m, 5, 7)
+            if m % CO_TILES == CO_TILES - 1:
+                finish_branch(m // CO_TILES)

@@ -1,7 +1,6 @@
 from contextlib import ExitStack
 
 import concourse.mybir as mybir
-from concourse.masks import make_identity
 
 BF16 = mybir.dt.bfloat16
 F32 = mybir.dt.float32
@@ -36,7 +35,9 @@ FIRST = (0, 512)
 MIDDLE = (512, 640)
 LAST = (640, 1152)
 
-VECTOR_COLS = 384
+VECTOR_COLS = (384, 480)
+
+GPSIMD_BANDS = 4
 
 FLOPS = 2 * BRANCHES * BATCH * CO * CHANNELS * POS
 
@@ -69,7 +70,9 @@ def tile_guided_cam_module2_pa_kernel(
     with ExitStack() as stack:
         keep = stack.enter_context(tc.tile_pool(name="keep", bufs=1))
         stage = stack.enter_context(tc.tile_pool(name="stage", bufs=4))
+        halves = stack.enter_context(tc.tile_pool(name="halves", bufs=1))
         psum = stack.enter_context(tc.psum_pool(name="psum", bufs=8))
+        stack.enter_context(tc.manual_schedule())
 
         raw = [
             [keep.tile([P, PACK, POS], BF16, name="raw%d%d" % (b, g)) for g in range(GROUPS)]
@@ -82,76 +85,73 @@ def tile_guided_cam_module2_pa_kernel(
         w_planes = keep.tile([P, BRANCHES, CO], U8, name="w_planes", align_bytes=64)
         x_words = keep.tile([P, GROUPS, COLS], U32, name="x_words", align_bytes=64)
         x_planes = keep.tile([P, GROUPS, COLS], U8, name="x_planes", align_bytes=64)
-        bn_rows = keep.tile([P, P], BF16, name="bn_rows")
-        ident = keep.tile([P, P], BF16, name="ident")
+        bn_rows = keep.tile([P, 32], BF16, name="bn_rows", align_bytes=64)
+        bn_cols = keep.tile([P, 32], BF16, name="bn_cols", align_bytes=64)
+        warm = keep.tile([P, 1], F32, name="warm")
         z = keep.tile([P, M_TILES, COLS], F32, name="z")
         cell_sums = keep.tile([P, M_TILES, BANDS * GRID], F32, name="cell_sums")
 
         nc.vector.memset(w_planes[:].bitcast(I32), 0)
-        nc.vector.memset(bn_rows[:], 0.0)
-        make_identity(nc, ident[:])
+        nc.vector.memset(warm[:], 1.0)
+        nc.scalar.sqrt(out=warm[:], in_=warm[:])
 
         def load_x(b, g):
             rows = x_rows[b, g * K_PASS : (g + 1) * K_PASS, :]
             nc.sync.dma_start(out=raw[b][g][:], in_=rows.rearrange("(p t) n -> p t n", t=PACK))
 
-        def load_words(g):
-            for br in range(BRANCHES):
-                nc.sync.dma_start(
-                    out=w_words[br][:, g, :].bitcast(I32),
-                    in_=words_in[br][g].rearrange("p n t -> p (n t)").bitcast(I32),
-                )
+        def load_words(br, g):
+            nc.sync.dma_start(
+                out=w_words[br][:, g, :].bitcast(I32),
+                in_=words_in[br][g].rearrange("p n t -> p (n t)").bitcast(I32),
+            )
 
-        load_x(0, 0)
-        load_words(0)
-        for br in range(BRANCHES):
+        def load_planes(br):
             for quad in range(4):
                 nc.sync.dma_start(
                     out=w_planes[32 * quad : 32 * quad + 16, br, :].bitcast(I32),
                     in_=scales_in[br][:, 4 * quad : 4 * quad + 4, :].bitcast(I32),
                 )
+
+        def load_bn(br):
+            for v in range(4 * br, 4 * br + 4):
+                nc.sync.dma_start(
+                    out=bn_rows[v : P : len(bn_in), :],
+                    in_=bn_in[v].rearrange("(c q i) -> q c i", c=CO_TILES, i=32),
+                )
+
+        load_x(0, 0)
+        load_planes(0)
+        load_words(0, 0)
+        load_words(1, 0)
         load_x(0, 1)
-        load_words(1)
-        for v in range(len(bn_in)):
-            nc.scalar.dma_start(
-                out=bn_rows[CO_TILES * v : CO_TILES * (v + 1), :],
-                in_=bn_in[v].rearrange("(c p) -> c p", p=P),
-            )
-        for g in range(2, GROUPS):
-            load_x(0, g)
-            load_words(g)
+        load_planes(1)
+        load_words(0, 1)
+        load_words(1, 1)
+        load_x(0, 2)
+        load_words(0, 2)
+        load_bn(0)
+        load_words(1, 2)
+        load_x(0, 3)
+        load_words(0, 3)
+        load_words(1, 3)
+        load_bn(1)
         for g in range(GROUPS):
             load_x(1, g)
 
-        bn_ps = psum.tile([P, P], BF16, tag="acc")
-        nc.tensor.transpose(bn_ps[:], bn_rows[:], ident[:])
-        bn = keep.tile([P, BRANCHES, 4, CO_TILES], F32, name="bn")
-        nc.vector.tensor_copy(
-            out=bn[:].rearrange("p b k c -> p (b k c)"), in_=bn_ps[:, 0 : BRANCHES * 4 * CO_TILES]
-        )
-        gain, bias, mean, var = [bn[:, :, kind, :] for kind in range(4)]
-        rstd = keep.tile([P, BRANCHES, CO_TILES], F32, name="rstd")
-        slope = keep.tile([P, BRANCHES, CO_TILES], F32, name="slope")
-        shift = keep.tile([P, BRANCHES, CO_TILES], F32, name="shift")
-        nc.vector.tensor_scalar_add(out=rstd[:], in0=var, scalar1=EPS)
-        nc.scalar.sqrt(out=rstd[:], in_=rstd[:])
-        nc.vector.reciprocal(out=rstd[:], in_=rstd[:])
-        nc.vector.tensor_mul(out=slope[:], in0=gain, in1=rstd[:])
-        nc.vector.tensor_mul(out=shift[:], in0=mean, in1=slope[:])
-        nc.vector.tensor_sub(out=shift[:], in0=bias, in1=shift[:])
-        slope_m = slope[:].rearrange("p b c -> p (b c)")
-        shift_m = shift[:].rearrange("p b c -> p (b c)")
-
-        def quantise_slab(b, g):
+        def regroup_slab(b, g):
             grouped = stage.tile([P, POS, PACK], BF16, tag="grouped", align_bytes=64)
+            cut = VECTOR_COLS[b]
             nc.vector.tensor_copy(
-                out=grouped[:, 0:VECTOR_COLS, :].rearrange("p (c i) t -> p c t i", i=4),
-                in_=raw[b][g][:, :, 0:VECTOR_COLS].rearrange("p t (c i) -> p c t i", i=4),
+                out=grouped[:, 0:cut, :].rearrange("p (c i) t -> p c t i", i=4),
+                in_=raw[b][g][:, :, 0:cut].rearrange("p t (c i) -> p c t i", i=4),
             )
             nc.scalar.copy(
-                out=grouped[:, VECTOR_COLS:POS, :].rearrange("p (c i) t -> p c t i", i=4),
-                in_=raw[b][g][:, :, VECTOR_COLS:POS].rearrange("p t (c i) -> p c t i", i=4),
+                out=grouped[:, cut:POS, :].rearrange("p (c i) t -> p c t i", i=4),
+                in_=raw[b][g][:, :, cut:POS].rearrange("p t (c i) -> p c t i", i=4),
             )
+            return grouped
+
+        def quantise_slab(b, g, grouped):
             cut = 512 if b == 0 else 64
             for lo, hi in ((0, cut), (cut, POS)):
                 nc.vector.quantize_mx(
@@ -198,6 +198,25 @@ def tile_guided_cam_module2_pa_kernel(
                 op=ADD,
             )
 
+        def pool_bands_gpsimd(lo, hi):
+            rows = z[:, lo:hi, 0 : GPSIMD_BANDS * BAND].rearrange("p m (r h) -> p m r h", h=BAND)
+            two_rows = halves.tile([P, hi - lo, GPSIMD_BANDS, 2 * SIDE], F32, name="two_rows")
+            one_row = halves.tile([P, hi - lo, GPSIMD_BANDS, SIDE], F32, name="one_row")
+            two_cols = halves.tile([P, hi - lo, GPSIMD_BANDS * GRID, 2], F32, name="two_cols")
+            nc.gpsimd.tensor_add(
+                out=two_rows[:], in0=rows[:, :, :, 0 : 2 * SIDE], in1=rows[:, :, :, 2 * SIDE : BAND]
+            )
+            nc.gpsimd.tensor_add(
+                out=one_row[:], in0=two_rows[:, :, :, 0:SIDE], in1=two_rows[:, :, :, SIDE : 2 * SIDE]
+            )
+            cells = one_row[:].rearrange("p m r (c j) -> p m (r c) j", j=CELL)
+            nc.gpsimd.tensor_add(out=two_cols[:], in0=cells[:, :, :, 0:2], in1=cells[:, :, :, 2:4])
+            nc.gpsimd.tensor_add(
+                out=cell_sums[:, lo:hi, 0 : GPSIMD_BANDS * GRID],
+                in0=two_cols[:, :, :, 0],
+                in1=two_cols[:, :, :, 1],
+            )
+
         def finish_branch(br):
             sums = cell_sums[:, br * CO_TILES : (br + 1) * CO_TILES, :]
             res = keep.tile([P, BATCH, CO_TILES, FEATS], F32, name="res%d" % br)
@@ -238,36 +257,59 @@ def tile_guided_cam_module2_pa_kernel(
                 in_=res[:].rearrange("p b m f -> p (b m) f"),
             )
 
-        accs = [new_acc(FIRST) for m in range(M_TILES)]
+        first_accs = [new_acc(FIRST) for m in range(M_TILES)]
         for g in range(GROUPS):
-            quantise_slab(0, g)
+            quantise_slab(0, g, regroup_slab(0, g))
             for m in range(M_TILES):
-                mx_pass(accs[m], m, g, FIRST)
-        for g in range(GROUPS):
-            quantise_slab(1, g)
-        for m in range(M_TILES):
-            bn_relu(accs[m], m, FIRST)
-            pool_bands(m, 0, 5)
+                mx_pass(first_accs[m], m, g, FIRST)
 
-        accs = [new_acc(LAST) for m in range(CO_TILES)]
-        for g in range(GROUPS):
-            for m in range(CO_TILES):
-                mx_pass(accs[m], m, g, LAST)
-        for m in range(CO_TILES):
-            bn_relu(accs[m], m, LAST)
-            pool_bands(m, 7, 12)
-        for m in range(CO_TILES, M_TILES):
-            acc = new_acc(LAST)
-            for g in range(GROUPS):
-                mx_pass(acc, m, g, LAST)
-            bn_relu(acc, m, LAST)
-            pool_bands(m, 7, 12)
+        nc.vector.transpose(out=bn_cols[:], in_=bn_rows[:])
+        by_kind = bn_cols[:].rearrange("p (c b k) -> p b k c", b=BRANCHES, k=4)
+        gain, bias, mean, var = [by_kind[:, :, kind, :] for kind in range(4)]
+        rstd = keep.tile([P, BRANCHES, CO_TILES], F32, name="rstd")
+        slope = keep.tile([P, BRANCHES, CO_TILES], F32, name="slope")
+        shift = keep.tile([P, BRANCHES, CO_TILES], F32, name="shift")
+        nc.vector.tensor_scalar_add(out=rstd[:], in0=var, scalar1=EPS)
+        nc.scalar.sqrt(out=rstd[:], in_=rstd[:])
+        nc.vector.reciprocal(out=rstd[:], in_=rstd[:])
+        nc.vector.tensor_mul(out=slope[:], in0=gain, in1=rstd[:])
+        nc.vector.tensor_mul(out=shift[:], in0=mean, in1=slope[:])
+        nc.vector.tensor_sub(out=shift[:], in0=bias, in1=shift[:])
+        slope_m = slope[:].rearrange("p b c -> p (b c)")
+        shift_m = shift[:].rearrange("p b c -> p (b c)")
 
-        for m in range(M_TILES):
+        q_tiles = range(CO_TILES)
+        last_accs = [new_acc(LAST) for m in q_tiles]
+        grouped_next = regroup_slab(1, 0)
+        for g in range(GROUPS):
+            grouped_now = grouped_next
+            if g + 1 < GROUPS:
+                grouped_next = regroup_slab(1, g + 1)
+            quantise_slab(1, g, grouped_now)
+            for m in (2 * g, 2 * g + 1):
+                bn_relu(first_accs[m], m, FIRST)
+            for m in q_tiles:
+                mx_pass(last_accs[m], m, g, LAST)
+        pool_bands_gpsimd(CO_TILES, M_TILES)
+
+        for m in q_tiles:
+            pool_bands(m, 0, GPSIMD_BANDS)
+        for m in q_tiles:
+            bn_relu(last_accs[m], m, LAST)
+            pool_bands(m, 7, 12)
+        for m in q_tiles:
             acc = new_acc(MIDDLE)
             for g in range(GROUPS):
                 mx_pass(acc, m, g, MIDDLE)
             bn_relu(acc, m, MIDDLE)
-            pool_bands(m, 5, 7)
-            if m % CO_TILES == CO_TILES - 1:
-                finish_branch(m // CO_TILES)
+            pool_bands(m, GPSIMD_BANDS, 7)
+        finish_branch(0)
+
+        for m in range(CO_TILES, M_TILES):
+            for cols, first_band, stop_band in ((LAST, 7, 12), (MIDDLE, GPSIMD_BANDS, 7)):
+                acc = new_acc(cols)
+                for g in range(GROUPS):
+                    mx_pass(acc, m, g, cols)
+                bn_relu(acc, m, cols)
+                pool_bands(m, first_band, stop_band)
+        finish_branch(1)

@@ -35,7 +35,7 @@ FIRST = (0, 512)
 MIDDLE = (512, 640)
 LAST = (640, 1152)
 
-VECTOR_COLS = (384, 480)
+VECTOR_COLS = (384, 384)
 
 GPSIMD_BANDS = 4
 
@@ -90,6 +90,10 @@ def tile_guided_cam_module2_pa_kernel(
         warm = keep.tile([P, 1], F32, name="warm")
         z = keep.tile([P, M_TILES, COLS], F32, name="z")
         cell_sums = keep.tile([P, M_TILES, BANDS * GRID], F32, name="cell_sums")
+
+        two_rows = halves.tile([P, CO_TILES, GPSIMD_BANDS, 2 * SIDE], F32, name="two_rows")
+        one_row = halves.tile([P, CO_TILES, GPSIMD_BANDS, SIDE], F32, name="one_row")
+        two_cols = halves.tile([P, CO_TILES, GPSIMD_BANDS * GRID, 2], F32, name="two_cols")
 
         nc.vector.memset(w_planes[:].bitcast(I32), 0)
         nc.vector.memset(warm[:], 1.0)
@@ -200,9 +204,6 @@ def tile_guided_cam_module2_pa_kernel(
 
         def pool_bands_gpsimd(lo, hi):
             rows = z[:, lo:hi, 0 : GPSIMD_BANDS * BAND].rearrange("p m (r h) -> p m r h", h=BAND)
-            two_rows = halves.tile([P, hi - lo, GPSIMD_BANDS, 2 * SIDE], F32, name="two_rows")
-            one_row = halves.tile([P, hi - lo, GPSIMD_BANDS, SIDE], F32, name="one_row")
-            two_cols = halves.tile([P, hi - lo, GPSIMD_BANDS * GRID, 2], F32, name="two_cols")
             nc.gpsimd.tensor_add(
                 out=two_rows[:], in0=rows[:, :, :, 0 : 2 * SIDE], in1=rows[:, :, :, 2 * SIDE : BAND]
             )
@@ -224,28 +225,28 @@ def tile_guided_cam_module2_pa_kernel(
             sums2 = keep.tile([P, CO_TILES, BATCH, 4], F32, name="sums2_%d" % br)
             sums1 = keep.tile([P, CO_TILES, BATCH, 1], F32, name="sums1_%d" % br)
             nc.vector.tensor_reduce(
-                out=sums3[:].rearrange("p m b (r c) -> p (m b r) c", c=3),
-                in_=sums.rearrange("p m (b r i c j) -> p (m b r) c i j", b=BATCH, r=3, i=2, c=3, j=2),
-                axis=mybir.AxisListType.XY,
-                op=ADD,
-            )
-            nc.vector.tensor_reduce(
                 out=sums2[:].rearrange("p m b (r c) -> p (m b r) c", c=2),
                 in_=sums.rearrange("p m (b r i c j) -> p (m b r) c i j", b=BATCH, r=2, i=3, c=2, j=3),
                 axis=mybir.AxisListType.XY,
                 op=ADD,
             )
             nc.vector.tensor_reduce(
+                out=sums3[:].rearrange("p m b (r c) -> p (m b r) c", c=3),
+                in_=sums.rearrange("p m (b r i c j) -> p (m b r) c i j", b=BATCH, r=3, i=2, c=3, j=2),
+                axis=mybir.AxisListType.XY,
+                op=ADD,
+            )
+            nc.vector.tensor_reduce(
                 out=sums1[:].rearrange("p m b o -> p (m b) o"),
-                in_=sums2[:].rearrange("p m b f -> p (m b) f"),
+                in_=sums.rearrange("p m (b f) -> p (m b) f", b=BATCH),
                 axis=mybir.AxisListType.X,
                 op=ADD,
             )
             for level_sums, first, side in (
-                (sums1[:], 0, 1),
+                (sums.rearrange("p m (b f) -> p m b f", b=BATCH), 14, 6),
                 (sums2[:], 1, 2),
                 (sums3[:], 5, 3),
-                (sums.rearrange("p m (b f) -> p m b f", b=BATCH), 14, 6),
+                (sums1[:], 0, 1),
             ):
                 nc.vector.tensor_scalar_mul(
                     out=res[:, :, :, first : first + side * side].rearrange("p b m f -> p m b f"),
@@ -269,18 +270,18 @@ def tile_guided_cam_module2_pa_kernel(
         rstd = keep.tile([P, BRANCHES, CO_TILES], F32, name="rstd")
         slope = keep.tile([P, BRANCHES, CO_TILES], F32, name="slope")
         shift = keep.tile([P, BRANCHES, CO_TILES], F32, name="shift")
-        nc.vector.tensor_scalar_add(out=rstd[:], in0=var, scalar1=EPS)
+        nc.gpsimd.tensor_scalar_add(out=rstd[:], in0=var, scalar1=EPS)
         nc.scalar.sqrt(out=rstd[:], in_=rstd[:])
-        nc.vector.reciprocal(out=rstd[:], in_=rstd[:])
-        nc.vector.tensor_mul(out=slope[:], in0=gain, in1=rstd[:])
-        nc.vector.tensor_mul(out=shift[:], in0=mean, in1=slope[:])
-        nc.vector.tensor_sub(out=shift[:], in0=bias, in1=shift[:])
         slope_m = slope[:].rearrange("p b c -> p (b c)")
         shift_m = shift[:].rearrange("p b c -> p (b c)")
 
         q_tiles = range(CO_TILES)
         last_accs = [new_acc(LAST) for m in q_tiles]
         grouped_next = regroup_slab(1, 0)
+        nc.vector.reciprocal(out=rstd[:], in_=rstd[:])
+        nc.gpsimd.tensor_mul(out=slope[:], in0=gain, in1=rstd[:])
+        nc.gpsimd.tensor_mul(out=shift[:], in0=mean, in1=slope[:])
+        nc.gpsimd.tensor_sub(out=shift[:], in0=bias, in1=shift[:])
         for g in range(GROUPS):
             grouped_now = grouped_next
             if g + 1 < GROUPS:
@@ -290,10 +291,10 @@ def tile_guided_cam_module2_pa_kernel(
                 bn_relu(first_accs[m], m, FIRST)
             for m in q_tiles:
                 mx_pass(last_accs[m], m, g, LAST)
+        nc.vector.memset(two_rows[:, 0, 0, 0:1], 0.0)
+        pool_bands_gpsimd(0, CO_TILES)
         pool_bands_gpsimd(CO_TILES, M_TILES)
 
-        for m in q_tiles:
-            pool_bands(m, 0, GPSIMD_BANDS)
         for m in q_tiles:
             bn_relu(last_accs[m], m, LAST)
             pool_bands(m, 7, 12)

@@ -116,13 +116,14 @@ def tile_guided_cam_module2_pa_kernel(
                     in_=scales_in[br][:, 4 * quad : 4 * quad + 4, :].bitcast(I32),
                 )
 
-        def load_bn(br):
+        def load_bn(br, queue):
             for v in range(4 * br, 4 * br + 4):
-                nc.sync.dma_start(
+                queue.dma_start(
                     out=bn_rows[v : P : len(bn_in), :],
                     in_=bn_in[v].rearrange("(c q i) -> q c i", c=CO_TILES, i=32),
                 )
 
+        load_bn(1, nc.gpsimd)
         load_x(0, 0)
         load_planes(0)
         load_words(0, 0)
@@ -133,12 +134,11 @@ def tile_guided_cam_module2_pa_kernel(
         load_words(1, 1)
         load_x(0, 2)
         load_words(0, 2)
-        load_bn(0)
+        load_bn(0, nc.sync)
         load_words(1, 2)
         load_x(0, 3)
         load_words(0, 3)
         load_words(1, 3)
-        load_bn(1)
         for g in range(GROUPS):
             load_x(1, g)
 
@@ -258,30 +258,32 @@ def tile_guided_cam_module2_pa_kernel(
                 in_=res[:].rearrange("p b m f -> p (b m) f"),
             )
 
-        first_accs = [new_acc(FIRST) for m in range(M_TILES)]
-        for g in range(GROUPS):
-            quantise_slab(0, g, regroup_slab(0, g))
-            for m in range(M_TILES):
-                mx_pass(first_accs[m], m, g, FIRST)
-
-        nc.vector.transpose(out=bn_cols[:], in_=bn_rows[:])
         by_kind = bn_cols[:].rearrange("p (c b k) -> p b k c", b=BRANCHES, k=4)
         gain, bias, mean, var = [by_kind[:, :, kind, :] for kind in range(4)]
         rstd = keep.tile([P, BRANCHES, CO_TILES], F32, name="rstd")
         slope = keep.tile([P, BRANCHES, CO_TILES], F32, name="slope")
         shift = keep.tile([P, BRANCHES, CO_TILES], F32, name="shift")
-        nc.gpsimd.tensor_scalar_add(out=rstd[:], in0=var, scalar1=EPS)
-        nc.scalar.sqrt(out=rstd[:], in_=rstd[:])
+        first_accs = [new_acc(FIRST) for m in range(M_TILES)]
+        for g in range(GROUPS):
+            grouped = regroup_slab(0, g)
+            if g == 3:
+                nc.vector.reciprocal(out=rstd[:], in_=rstd[:])
+            quantise_slab(0, g, grouped)
+            for m in range(M_TILES):
+                mx_pass(first_accs[m], m, g, FIRST)
+            if g == 2:
+                nc.vector.transpose(out=bn_cols[:], in_=bn_rows[:])
+                nc.vector.tensor_scalar_add(out=rstd[:], in0=var, scalar1=EPS)
+                nc.scalar.sqrt(out=rstd[:], in_=rstd[:])
+        nc.vector.tensor_mul(out=slope[:], in0=gain, in1=rstd[:])
+        nc.vector.tensor_mul(out=shift[:], in0=mean, in1=slope[:])
         slope_m = slope[:].rearrange("p b c -> p (b c)")
         shift_m = shift[:].rearrange("p b c -> p (b c)")
 
         q_tiles = range(CO_TILES)
         last_accs = [new_acc(LAST) for m in q_tiles]
         grouped_next = regroup_slab(1, 0)
-        nc.vector.reciprocal(out=rstd[:], in_=rstd[:])
-        nc.gpsimd.tensor_mul(out=slope[:], in0=gain, in1=rstd[:])
-        nc.gpsimd.tensor_mul(out=shift[:], in0=mean, in1=slope[:])
-        nc.gpsimd.tensor_sub(out=shift[:], in0=bias, in1=shift[:])
+        nc.vector.tensor_sub(out=shift[:], in0=bias, in1=shift[:])
         for g in range(GROUPS):
             grouped_now = grouped_next
             if g + 1 < GROUPS:

@@ -39,6 +39,8 @@ VECTOR_COLS = (384, 384)
 
 GPSIMD_BANDS = 4
 
+VECTOR_FIRST_TILES = 2
+
 FLOPS = 2 * BRANCHES * BATCH * CO * CHANNELS * POS
 
 
@@ -142,27 +144,28 @@ def tile_guided_cam_module2_pa_kernel(
         for g in range(GROUPS):
             load_x(1, g)
 
+        def regroup_cols(engine_copy, b, g, grouped, lo, hi):
+            engine_copy(
+                out=grouped[:, lo:hi, :].rearrange("p (c i) t -> p c t i", i=4),
+                in_=raw[b][g][:, :, lo:hi].rearrange("p t (c i) -> p c t i", i=4),
+            )
+
         def regroup_slab(b, g):
             grouped = stage.tile([P, POS, PACK], BF16, tag="grouped", align_bytes=64)
-            cut = VECTOR_COLS[b]
-            nc.vector.tensor_copy(
-                out=grouped[:, 0:cut, :].rearrange("p (c i) t -> p c t i", i=4),
-                in_=raw[b][g][:, :, 0:cut].rearrange("p t (c i) -> p c t i", i=4),
-            )
-            nc.scalar.copy(
-                out=grouped[:, cut:POS, :].rearrange("p (c i) t -> p c t i", i=4),
-                in_=raw[b][g][:, :, cut:POS].rearrange("p t (c i) -> p c t i", i=4),
-            )
+            if b == 0:
+                regroup_cols(nc.vector.tensor_copy, b, g, grouped, 0, VECTOR_COLS[b])
+                regroup_cols(nc.scalar.copy, b, g, grouped, VECTOR_COLS[b], POS)
+            else:
+                regroup_cols(nc.vector.tensor_copy, b, g, grouped, POS - VECTOR_COLS[b], POS)
+                regroup_cols(nc.scalar.copy, b, g, grouped, 64, POS - VECTOR_COLS[b])
             return grouped
 
-        def quantise_slab(b, g, grouped):
-            cut = 512 if b == 0 else 64
-            for lo, hi in ((0, cut), (cut, POS)):
-                nc.vector.quantize_mx(
-                    out=x_words[:, g, b * POS + lo : b * POS + hi].bitcast(FP8X4),
-                    scales=x_planes[:, g, b * POS + lo : b * POS + hi],
-                    in_=grouped[:, lo:hi, :].rearrange("p n t -> p (n t)"),
-                )
+        def quantise_cols(b, g, grouped, lo, hi):
+            nc.vector.quantize_mx(
+                out=x_words[:, g, b * POS + lo : b * POS + hi].bitcast(FP8X4),
+                scales=x_planes[:, g, b * POS + lo : b * POS + hi],
+                in_=grouped[:, lo:hi, :].rearrange("p n t -> p (n t)"),
+            )
 
         def mx_pass(acc, m, g, cols):
             br, co = divmod(m, CO_TILES)
@@ -204,26 +207,31 @@ def tile_guided_cam_module2_pa_kernel(
 
         def pool_bands_gpsimd(lo, hi):
             rows = z[:, lo:hi, 0 : GPSIMD_BANDS * BAND].rearrange("p m (r h) -> p m r h", h=BAND)
+            n = hi - lo
             nc.gpsimd.tensor_add(
-                out=two_rows[:], in0=rows[:, :, :, 0 : 2 * SIDE], in1=rows[:, :, :, 2 * SIDE : BAND]
+                out=two_rows[:, 0:n], in0=rows[:, :, :, 0 : 2 * SIDE], in1=rows[:, :, :, 2 * SIDE : BAND]
             )
             nc.gpsimd.tensor_add(
-                out=one_row[:], in0=two_rows[:, :, :, 0:SIDE], in1=two_rows[:, :, :, SIDE : 2 * SIDE]
+                out=one_row[:, 0:n],
+                in0=two_rows[:, 0:n, :, 0:SIDE],
+                in1=two_rows[:, 0:n, :, SIDE : 2 * SIDE],
             )
-            cells = one_row[:].rearrange("p m r (c j) -> p m (r c) j", j=CELL)
-            nc.gpsimd.tensor_add(out=two_cols[:], in0=cells[:, :, :, 0:2], in1=cells[:, :, :, 2:4])
+            cells = one_row[:, 0:n].rearrange("p m r (c j) -> p m (r c) j", j=CELL)
+            nc.gpsimd.tensor_add(
+                out=two_cols[:, 0:n], in0=cells[:, :, :, 0:2], in1=cells[:, :, :, 2:4]
+            )
             nc.gpsimd.tensor_add(
                 out=cell_sums[:, lo:hi, 0 : GPSIMD_BANDS * GRID],
-                in0=two_cols[:, :, :, 0],
-                in1=two_cols[:, :, :, 1],
+                in0=two_cols[:, 0:n, :, 0],
+                in1=two_cols[:, 0:n, :, 1],
             )
 
-        def finish_branch(br):
-            sums = cell_sums[:, br * CO_TILES : (br + 1) * CO_TILES, :]
-            res = keep.tile([P, BATCH, CO_TILES, FEATS], F32, name="res%d" % br)
-            sums3 = keep.tile([P, CO_TILES, BATCH, 9], F32, name="sums3_%d" % br)
-            sums2 = keep.tile([P, CO_TILES, BATCH, 4], F32, name="sums2_%d" % br)
-            sums1 = keep.tile([P, CO_TILES, BATCH, 1], F32, name="sums1_%d" % br)
+        def coarser_sums(lo, hi):
+            n = hi - lo
+            sums = cell_sums[:, lo:hi, :]
+            sums3 = keep.tile([P, n, BATCH, 9], F32, name="sums3_%d" % lo)
+            sums2 = keep.tile([P, n, BATCH, 4], F32, name="sums2_%d" % lo)
+            sums1 = keep.tile([P, n, BATCH, 1], F32, name="sums1_%d" % lo)
             nc.vector.tensor_reduce(
                 out=sums2[:].rearrange("p m b (r c) -> p (m b r) c", c=2),
                 in_=sums.rearrange("p m (b r i c j) -> p (m b r) c i j", b=BATCH, r=2, i=3, c=2, j=3),
@@ -242,21 +250,38 @@ def tile_guided_cam_module2_pa_kernel(
                 axis=mybir.AxisListType.X,
                 op=ADD,
             )
-            for level_sums, first, side in (
+            return (
                 (sums.rearrange("p m (b f) -> p m b f", b=BATCH), 14, 6),
                 (sums2[:], 1, 2),
                 (sums3[:], 5, 3),
                 (sums1[:], 0, 1),
-            ):
-                nc.vector.tensor_scalar_mul(
-                    out=res[:, :, :, first : first + side * side].rearrange("p b m f -> p m b f"),
-                    in0=level_sums,
-                    scalar1=float(side * side) / POS,
-                )
-            nc.sync.dma_start(
-                out=outs[br].rearrange("b (m p) f -> p (b m) f", p=P),
-                in_=res[:].rearrange("p b m f -> p (b m) f"),
             )
+
+        def scale_and_store(lo, hi, levels, on_scalar):
+            n = hi - lo
+            br, first_tile = divmod(lo, CO_TILES)
+            res = keep.tile([P, BATCH, n, FEATS], F32, name="res%d" % lo)
+            for level_sums, first, side in levels:
+                means = res[:, :, :, first : first + side * side].rearrange("p b m f -> p m b f")
+                if on_scalar:
+                    nc.scalar.mul(out=means, in_=level_sums, mul=float(side * side) / POS)
+                else:
+                    nc.vector.tensor_scalar_mul(
+                        out=means, in0=level_sums, scalar1=float(side * side) / POS
+                    )
+            rows = outs[br].rearrange("b (m p) f -> p b m f", p=P)
+            if n == CO_TILES:
+                nc.sync.dma_start(
+                    out=outs[br].rearrange("b (m p) f -> p (b m) f", p=P),
+                    in_=res[:].rearrange("p b m f -> p (b m) f"),
+                )
+            elif n == 1:
+                nc.sync.dma_start(out=rows[:, :, first_tile, :], in_=res[:, :, 0, :])
+            else:
+                for b in range(BATCH):
+                    nc.sync.dma_start(
+                        out=rows[:, b, first_tile : first_tile + n, :], in_=res[:, b, :, :]
+                    )
 
         by_kind = bn_cols[:].rearrange("p (c b k) -> p b k c", b=BRANCHES, k=4)
         gain, bias, mean, var = [by_kind[:, :, kind, :] for kind in range(4)]
@@ -268,7 +293,8 @@ def tile_guided_cam_module2_pa_kernel(
             grouped = regroup_slab(0, g)
             if g == 3:
                 nc.vector.reciprocal(out=rstd[:], in_=rstd[:])
-            quantise_slab(0, g, grouped)
+            quantise_cols(0, g, grouped, 0, 512)
+            quantise_cols(0, g, grouped, 512, POS)
             for m in range(M_TILES):
                 mx_pass(first_accs[m], m, g, FIRST)
             if g == 2:
@@ -282,20 +308,25 @@ def tile_guided_cam_module2_pa_kernel(
 
         q_tiles = range(CO_TILES)
         last_accs = [new_acc(LAST) for m in q_tiles]
-        grouped_next = regroup_slab(1, 0)
+        grouped_1 = [regroup_slab(1, 0)]
         nc.vector.tensor_sub(out=shift[:], in0=bias, in1=shift[:])
         for g in range(GROUPS):
-            grouped_now = grouped_next
             if g + 1 < GROUPS:
-                grouped_next = regroup_slab(1, g + 1)
-            quantise_slab(1, g, grouped_now)
+                grouped_1.append(regroup_slab(1, g + 1))
+            quantise_cols(1, g, grouped_1[g], 64, POS)
             for m in (2 * g, 2 * g + 1):
                 bn_relu(first_accs[m], m, FIRST)
             for m in q_tiles:
                 mx_pass(last_accs[m], m, g, LAST)
+        for g in range(GROUPS):
+            regroup_cols(nc.vector.tensor_copy, 1, g, grouped_1[g], 0, 64)
+        for g in range(GROUPS):
+            quantise_cols(1, g, grouped_1[g], 0, 64)
         nc.vector.memset(two_rows[:, 0, 0, 0:1], 0.0)
-        pool_bands_gpsimd(0, CO_TILES)
+        pool_bands_gpsimd(VECTOR_FIRST_TILES, CO_TILES)
         pool_bands_gpsimd(CO_TILES, M_TILES)
+        for m in range(VECTOR_FIRST_TILES):
+            pool_bands(m, 0, GPSIMD_BANDS)
 
         for m in q_tiles:
             bn_relu(last_accs[m], m, LAST)
@@ -306,13 +337,21 @@ def tile_guided_cam_module2_pa_kernel(
                 mx_pass(acc, m, g, MIDDLE)
             bn_relu(acc, m, MIDDLE)
             pool_bands(m, GPSIMD_BANDS, 7)
-        finish_branch(0)
+        q_levels = coarser_sums(0, CO_TILES)
 
+        last_tile = M_TILES - 1
         for m in range(CO_TILES, M_TILES):
-            for cols, first_band, stop_band in ((LAST, 7, 12), (MIDDLE, GPSIMD_BANDS, 7)):
+            for cols in (LAST, MIDDLE):
                 acc = new_acc(cols)
                 for g in range(GROUPS):
                     mx_pass(acc, m, g, cols)
                 bn_relu(acc, m, cols)
-                pool_bands(m, first_band, stop_band)
-        finish_branch(1)
+                if m == last_tile and cols == LAST:
+                    pool_bands(m, 7, 12)
+            pool_bands(m, GPSIMD_BANDS, 7 if m == last_tile else 12)
+            if m == CO_TILES + 1:
+                scale_and_store(0, CO_TILES, q_levels, True)
+            if m == last_tile - 1:
+                k_levels = coarser_sums(CO_TILES, last_tile)
+        scale_and_store(CO_TILES, last_tile, k_levels, True)
+        scale_and_store(last_tile, M_TILES, coarser_sums(last_tile, M_TILES), False)

@@ -71,7 +71,7 @@ def tile_guided_cam_module2_pa_kernel(
 
     with ExitStack() as stack:
         keep = stack.enter_context(tc.tile_pool(name="keep", bufs=1))
-        stage = stack.enter_context(tc.tile_pool(name="stage", bufs=4))
+        stage = stack.enter_context(tc.tile_pool(name="stage", bufs=5))
         halves = stack.enter_context(tc.tile_pool(name="halves", bufs=1))
         psum = stack.enter_context(tc.psum_pool(name="psum", bufs=8))
         stack.enter_context(tc.manual_schedule())
@@ -93,7 +93,6 @@ def tile_guided_cam_module2_pa_kernel(
         z = keep.tile([P, M_TILES, COLS], F32, name="z")
         cell_sums = keep.tile([P, M_TILES, BANDS * GRID], F32, name="cell_sums")
 
-        two_rows = halves.tile([P, CO_TILES, GPSIMD_BANDS, 2 * SIDE], F32, name="two_rows")
         one_row = halves.tile([P, CO_TILES, GPSIMD_BANDS, SIDE], F32, name="one_row")
         two_cols = halves.tile([P, CO_TILES, GPSIMD_BANDS * GRID, 2], F32, name="two_cols")
 
@@ -129,20 +128,22 @@ def tile_guided_cam_module2_pa_kernel(
         load_x(0, 0)
         load_planes(0)
         load_words(0, 0)
-        load_words(1, 0)
         load_x(0, 1)
+        load_words(1, 0)
         load_planes(1)
+        load_x(0, 2)
         load_words(0, 1)
         load_words(1, 1)
-        load_x(0, 2)
-        load_words(0, 2)
         load_bn(0, nc.sync)
-        load_words(1, 2)
         load_x(0, 3)
+        load_words(0, 2)
+        load_words(1, 2)
+        load_x(1, 0)
         load_words(0, 3)
+        load_x(1, 1)
         load_words(1, 3)
-        for g in range(GROUPS):
-            load_x(1, g)
+        load_x(1, 2)
+        load_x(1, 3)
 
         def regroup_cols(engine_copy, b, g, grouped, lo, hi):
             engine_copy(
@@ -294,15 +295,17 @@ def tile_guided_cam_module2_pa_kernel(
             if g == 3:
                 nc.vector.reciprocal(out=rstd[:], in_=rstd[:])
             quantise_cols(0, g, grouped, 0, 512)
-            quantise_cols(0, g, grouped, 512, POS)
+            if g < GROUPS - 1:
+                quantise_cols(0, g, grouped, 512, POS)
             for m in range(M_TILES):
                 mx_pass(first_accs[m], m, g, FIRST)
             if g == 2:
                 nc.vector.transpose(out=bn_cols[:], in_=bn_rows[:])
                 nc.vector.tensor_scalar_add(out=rstd[:], in0=var, scalar1=EPS)
                 nc.scalar.sqrt(out=rstd[:], in_=rstd[:])
+                nc.vector.tensor_mul(out=shift[:], in0=mean, in1=gain)
+        nc.vector.tensor_mul(out=shift[:], in0=shift[:], in1=rstd[:])
         nc.vector.tensor_mul(out=slope[:], in0=gain, in1=rstd[:])
-        nc.vector.tensor_mul(out=shift[:], in0=mean, in1=slope[:])
         slope_m = slope[:].rearrange("p b c -> p (b c)")
         shift_m = shift[:].rearrange("p b c -> p (b c)")
 
@@ -322,7 +325,10 @@ def tile_guided_cam_module2_pa_kernel(
             regroup_cols(nc.vector.tensor_copy, 1, g, grouped_1[g], 0, 64)
         for g in range(GROUPS):
             quantise_cols(1, g, grouped_1[g], 0, 64)
-        nc.vector.memset(two_rows[:, 0, 0, 0:1], 0.0)
+        quantise_cols(0, GROUPS - 1, grouped, 512, POS)
+        two_rows = stage.tile(
+            [P, CO_TILES, GPSIMD_BANDS, 2 * SIDE], F32, tag="grouped", align_bytes=64
+        )
         pool_bands_gpsimd(VECTOR_FIRST_TILES, CO_TILES)
         pool_bands_gpsimd(CO_TILES, M_TILES)
         for m in range(VECTOR_FIRST_TILES):

@@ -34,6 +34,8 @@ FEATS = 50
 FIRST = (0, 512)
 MIDDLE = (512, 640)
 LAST = (640, 1152)
+LAST_A = (640, 896)
+LAST_B = (896, 1152)
 
 VECTOR_COLS = (384, 384)
 
@@ -346,18 +348,23 @@ def tile_guided_cam_module2_pa_kernel(
         q_levels = coarser_sums(0, CO_TILES)
 
         last_tile = M_TILES - 1
-        for m in range(CO_TILES, M_TILES):
+        for m in range(CO_TILES, last_tile):
             for cols in (LAST, MIDDLE):
                 acc = new_acc(cols)
                 for g in range(GROUPS):
                     mx_pass(acc, m, g, cols)
                 bn_relu(acc, m, cols)
-                if m == last_tile and cols == LAST:
-                    pool_bands(m, 7, 12)
-            pool_bands(m, GPSIMD_BANDS, 7 if m == last_tile else 12)
+            pool_bands(m, GPSIMD_BANDS, 12)
             if m == CO_TILES + 1:
                 scale_and_store(0, CO_TILES, q_levels, True)
             if m == last_tile - 1:
                 k_levels = coarser_sums(CO_TILES, last_tile)
+        for cols, first_band, stop_band in ((MIDDLE, 0, 0), (LAST_A, GPSIMD_BANDS, 9), (LAST_B, 9, 12)):
+            acc = new_acc(cols)
+            for g in range(GROUPS):
+                mx_pass(acc, last_tile, g, cols)
+            bn_relu(acc, last_tile, cols)
+            if stop_band > first_band:
+                pool_bands(last_tile, first_band, stop_band)
         scale_and_store(CO_TILES, last_tile, k_levels, True)
         scale_and_store(last_tile, M_TILES, coarser_sums(last_tile, M_TILES), False)

@@ -249,7 +249,11 @@ def tile_guided_cam_module2_pa_kernel(
             )
             nc.vector.tensor_reduce(
                 out=sums1[:].rearrange("p m b o -> p (m b) o"),
-                in_=sums.rearrange("p m (b f) -> p (m b) f", b=BATCH),
+                in_=(
+                    sums2[:].rearrange("p m b f -> p (m b) f")
+                    if n > 1
+                    else sums.rearrange("p m (b f) -> p (m b) f", b=BATCH)
+                ),
                 axis=mybir.AxisListType.X,
                 op=ADD,
             )
@@ -355,8 +359,6 @@ def tile_guided_cam_module2_pa_kernel(
                     mx_pass(acc, m, g, cols)
                 bn_relu(acc, m, cols)
             pool_bands(m, GPSIMD_BANDS, 12)
-            if m == CO_TILES + 1:
-                scale_and_store(0, CO_TILES, q_levels, True)
             if m == last_tile - 1:
                 k_levels = coarser_sums(CO_TILES, last_tile)
         for cols, first_band, stop_band in ((MIDDLE, 0, 0), (LAST_A, GPSIMD_BANDS, 9), (LAST_B, 9, 12)):
@@ -366,5 +368,6 @@ def tile_guided_cam_module2_pa_kernel(
             bn_relu(acc, last_tile, cols)
             if stop_band > first_band:
                 pool_bands(last_tile, first_band, stop_band)
+        scale_and_store(0, CO_TILES, q_levels, True)
         scale_and_store(CO_TILES, last_tile, k_levels, True)
         scale_and_store(last_tile, M_TILES, coarser_sums(last_tile, M_TILES), False)

@@ -1,6 +1,7 @@
 from contextlib import ExitStack
 
 import concourse.mybir as mybir
+from concourse.masks import make_identity
 
 BF16 = mybir.dt.bfloat16
 F32 = mybir.dt.float32
@@ -30,6 +31,11 @@ BAND = CELL * SIDE
 BANDS = COLS // BAND
 EPS = 1e-5
 FEATS = 50
+
+GROUP = 4
+EDGE = 6
+ROW = EDGE + FEATS
+CUTS = ((EDGE, 48), (EDGE - 2, 48), (EDGE - 4, 48), (0, ROW))
 
 FIRST = (0, 512)
 MIDDLE = (512, 640)
@@ -93,6 +99,11 @@ def tile_guided_cam_module2_pa_kernel(
         bn_cols = keep.tile([P, 32], BF16, name="bn_cols", align_bytes=64)
         warm = keep.tile([P, 1], F32, name="warm")
         z = keep.tile([P, M_TILES, COLS], F32, name="z")
+        down_one = keep.tile([P, P + 1], F32, name="down_one")
+        rows_out = [
+            keep.tile([P, BATCH, CO_TILES, ROW], F32, name="rows_out%d" % br, align_bytes=64)
+            for br in range(BRANCHES)
+        ]
         cell_sums = keep.tile([P, M_TILES, BANDS * GRID], F32, name="cell_sums")
 
         one_row = halves.tile([P, CO_TILES, GPSIMD_BANDS, SIDE], F32, name="one_row")
@@ -127,6 +138,8 @@ def tile_guided_cam_module2_pa_kernel(
                 )
 
         load_bn(1, nc.gpsimd)
+        nc.gpsimd.memset(down_one[:, 0:1], 0.0)
+        make_identity(nc, down_one[:, 1 : P + 1])
         load_x(0, 0)
         load_planes(0)
         load_words(0, 0)
@@ -264,31 +277,49 @@ def tile_guided_cam_module2_pa_kernel(
                 (sums1[:], 0, 1),
             )
 
-        def scale_and_store(lo, hi, levels, on_scalar):
-            n = hi - lo
+        def scale(lo, hi, levels, on_scalar):
             br, first_tile = divmod(lo, CO_TILES)
-            res = keep.tile([P, BATCH, n, FEATS], F32, name="res%d" % lo)
+            res = rows_out[br][:, :, first_tile : first_tile + hi - lo, :]
             for level_sums, first, side in levels:
-                means = res[:, :, :, first : first + side * side].rearrange("p b m f -> p m b f")
+                means = res[:, :, :, EDGE + first : EDGE + first + side * side]
+                means = means.rearrange("p b m f -> p m b f")
                 if on_scalar:
                     nc.scalar.mul(out=means, in_=level_sums, mul=float(side * side) / POS)
                 else:
                     nc.vector.tensor_scalar_mul(
                         out=means, in0=level_sums, scalar1=float(side * side) / POS
                     )
-            rows = outs[br].rearrange("b (m p) f -> p b m f", p=P)
-            if n == CO_TILES:
+
+        def neighbours_ends(br):
+            tiles = slice(br * CO_TILES, (br + 1) * CO_TILES)
+            n = CO_TILES * BATCH
+            acc = psum.tile([P, 512], F32, tag="acc")
+            nc.tensor.matmul(
+                out=acc[:, 0 : n * EDGE].rearrange("p (k f) -> p k f", f=EDGE),
+                lhsT=down_one[:, 0:P],
+                rhs=cell_sums[:, tiles, :].rearrange("p m (b f) -> p (m b) f", b=BATCH)[
+                    :, :, GRID * (GRID - 1) : GRID * GRID
+                ],
+                start=True,
+                stop=True,
+            )
+            nc.scalar.mul(
+                out=rows_out[br][:, :, :, 0:EDGE].rearrange("p b m f -> p m b f"),
+                in_=acc[:, 0 : n * EDGE].rearrange("p (m b f) -> p m b f", b=BATCH, f=EDGE),
+                mul=float(GRID * GRID) / POS,
+            )
+
+        def store(br):
+            rows = outs[br].rearrange("b (m i r) f -> i (b m) (r f)", i=P // GROUP, r=GROUP)
+            done = 0
+            for r, (first, count) in enumerate(CUTS):
                 nc.sync.dma_start(
-                    out=outs[br].rearrange("b (m p) f -> p (b m) f", p=P),
-                    in_=res[:].rearrange("p b m f -> p (b m) f"),
+                    out=rows[:, :, done : done + count],
+                    in_=rows_out[br][r:P:GROUP, :, :, first : first + count].rearrange(
+                        "i b m f -> i (b m) f"
+                    ),
                 )
-            elif n == 1:
-                nc.sync.dma_start(out=rows[:, :, first_tile, :], in_=res[:, :, 0, :])
-            else:
-                for b in range(BATCH):
-                    nc.sync.dma_start(
-                        out=rows[:, b, first_tile : first_tile + n, :], in_=res[:, b, :, :]
-                    )
+                done += count
 
         by_kind = bn_cols[:].rearrange("p (c b k) -> p b k c", b=BRANCHES, k=4)
         gain, bias, mean, var = [by_kind[:, :, kind, :] for kind in range(4)]
@@ -360,6 +391,9 @@ def tile_guided_cam_module2_pa_kernel(
                 bn_relu(acc, m, cols)
             pool_bands(m, GPSIMD_BANDS, 12)
             if m == last_tile - 1:
+                neighbours_ends(0)
+                scale(0, CO_TILES, q_levels, True)
+                store(0)
                 k_levels = coarser_sums(CO_TILES, last_tile)
         for cols, first_band, stop_band in ((MIDDLE, 0, 0), (LAST_A, GPSIMD_BANDS, 9), (LAST_B, 9, 12)):
             acc = new_acc(cols)
@@ -368,6 +402,7 @@ def tile_guided_cam_module2_pa_kernel(
             bn_relu(acc, last_tile, cols)
             if stop_band > first_band:
                 pool_bands(last_tile, first_band, stop_band)
-        scale_and_store(0, CO_TILES, q_levels, True)
-        scale_and_store(CO_TILES, last_tile, k_levels, True)
-        scale_and_store(last_tile, M_TILES, coarser_sums(last_tile, M_TILES), False)
+        scale(CO_TILES, last_tile, k_levels, True)
+        neighbours_ends(1)
+        scale(last_tile, M_TILES, coarser_sums(last_tile, M_TILES), False)
+        store(1)

@@ -49,6 +49,11 @@ GPSIMD_BANDS = 4
 
 VECTOR_FIRST_TILES = 2
 
+BANKS_BEFORE_SLAB = (0, 2, 1, 1)
+
+WARM_MATMULS = 20
+WARM_COLS = 256
+
 FLOPS = 2 * BRANCHES * BATCH * CO * CHANNELS * POS
 
 
@@ -110,6 +115,13 @@ def tile_guided_cam_module2_pa_kernel(
         two_cols = halves.tile([P, CO_TILES, GPSIMD_BANDS * GRID, 2], F32, name="two_cols")
 
         nc.vector.memset(w_planes[:].bitcast(I32), 0)
+        warm_in = keep.tile([P, WARM_COLS], BF16, name="warm_in")
+        nc.vector.memset(warm_in[:], 0.0)
+        warm_acc = psum.tile([P, 512], F32, tag="acc", name="warm_acc")
+        for i in range(WARM_MATMULS):
+            nc.tensor.matmul(
+                out=warm_acc[:, 0:WARM_COLS], lhsT=warm_in[:, 0:P], rhs=warm_in[:], start=True, stop=True
+            )
         nc.vector.memset(warm[:], 1.0)
         nc.scalar.sqrt(out=warm[:], in_=warm[:])
 
@@ -166,15 +178,8 @@ def tile_guided_cam_module2_pa_kernel(
                 in_=raw[b][g][:, :, lo:hi].rearrange("p t (c i) -> p c t i", i=4),
             )
 
-        def regroup_slab(b, g):
-            grouped = stage.tile([P, POS, PACK], BF16, tag="grouped", align_bytes=64)
-            if b == 0:
-                regroup_cols(nc.vector.tensor_copy, b, g, grouped, 0, VECTOR_COLS[b])
-                regroup_cols(nc.scalar.copy, b, g, grouped, VECTOR_COLS[b], POS)
-            else:
-                regroup_cols(nc.vector.tensor_copy, b, g, grouped, POS - VECTOR_COLS[b], POS)
-                regroup_cols(nc.scalar.copy, b, g, grouped, 64, POS - VECTOR_COLS[b])
-            return grouped
+        def new_grouped():
+            return stage.tile([P, POS, PACK], BF16, tag="grouped", align_bytes=64, name="grouped")
 
         def quantise_cols(b, g, grouped, lo, hi):
             nc.vector.quantize_mx(
@@ -290,21 +295,22 @@ def tile_guided_cam_module2_pa_kernel(
                         out=means, in0=level_sums, scalar1=float(side * side) / POS
                     )
 
-        def neighbours_ends(br):
-            tiles = slice(br * CO_TILES, (br + 1) * CO_TILES)
-            n = CO_TILES * BATCH
+        def neighbours_ends(lo, hi):
+            br, first_tile = divmod(lo, CO_TILES)
+            n = (hi - lo) * BATCH
+            res = rows_out[br][:, :, first_tile : first_tile + hi - lo, 0:EDGE]
             acc = psum.tile([P, 512], F32, tag="acc")
             nc.tensor.matmul(
                 out=acc[:, 0 : n * EDGE].rearrange("p (k f) -> p k f", f=EDGE),
                 lhsT=down_one[:, 0:P],
-                rhs=cell_sums[:, tiles, :].rearrange("p m (b f) -> p (m b) f", b=BATCH)[
+                rhs=cell_sums[:, lo:hi, :].rearrange("p m (b f) -> p (m b) f", b=BATCH)[
                     :, :, GRID * (GRID - 1) : GRID * GRID
                 ],
                 start=True,
                 stop=True,
             )
             nc.scalar.mul(
-                out=rows_out[br][:, :, :, 0:EDGE].rearrange("p b m f -> p m b f"),
+                out=res.rearrange("p b m f -> p m b f"),
                 in_=acc[:, 0 : n * EDGE].rearrange("p (m b f) -> p m b f", b=BATCH, f=EDGE),
                 mul=float(GRID * GRID) / POS,
             )
@@ -328,7 +334,9 @@ def tile_guided_cam_module2_pa_kernel(
         shift = keep.tile([P, BRANCHES, CO_TILES], F32, name="shift")
         first_accs = [new_acc(FIRST) for m in range(M_TILES)]
         for g in range(GROUPS):
-            grouped = regroup_slab(0, g)
+            grouped = new_grouped()
+            regroup_cols(nc.vector.tensor_copy, 0, g, grouped, 0, VECTOR_COLS[0])
+            regroup_cols(nc.scalar.copy, 0, g, grouped, VECTOR_COLS[0], POS)
             if g == 3:
                 nc.vector.reciprocal(out=rstd[:], in_=rstd[:])
             quantise_cols(0, g, grouped, 0, 512)
@@ -348,18 +356,25 @@ def tile_guided_cam_module2_pa_kernel(
 
         q_tiles = range(CO_TILES)
         last_accs = [new_acc(LAST) for m in q_tiles]
-        grouped_1 = [regroup_slab(1, 0)]
-        nc.vector.tensor_sub(out=shift[:], in0=bias, in1=shift[:])
+        grouped_1 = []
+        emptied = 0
         for g in range(GROUPS):
-            if g + 1 < GROUPS:
-                grouped_1.append(regroup_slab(1, g + 1))
-            quantise_cols(1, g, grouped_1[g], 64, POS)
-            for m in (2 * g, 2 * g + 1):
+            grouped_1.append(new_grouped())
+            regroup_cols(nc.vector.tensor_copy, 1, g, grouped_1[g], POS - VECTOR_COLS[1], POS)
+            if g == 0:
+                nc.vector.tensor_sub(out=shift[:], in0=bias, in1=shift[:])
+            for m in range(emptied, emptied + BANKS_BEFORE_SLAB[g]):
                 bn_relu(first_accs[m], m, FIRST)
+            emptied += BANKS_BEFORE_SLAB[g]
+            regroup_cols(nc.scalar.copy, 1, g, grouped_1[g], 64, POS - VECTOR_COLS[1])
+            if g > 0:
+                regroup_cols(nc.vector.tensor_copy, 1, g - 1, grouped_1[g - 1], 0, 64)
+            quantise_cols(1, g, grouped_1[g], 64, POS)
             for m in q_tiles:
                 mx_pass(last_accs[m], m, g, LAST)
-        for g in range(GROUPS):
-            regroup_cols(nc.vector.tensor_copy, 1, g, grouped_1[g], 0, 64)
+        for m in range(emptied, M_TILES):
+            bn_relu(first_accs[m], m, FIRST)
+        regroup_cols(nc.vector.tensor_copy, 1, GROUPS - 1, grouped_1[GROUPS - 1], 0, 64)
         for g in range(GROUPS):
             quantise_cols(1, g, grouped_1[g], 0, 64)
         quantise_cols(0, GROUPS - 1, grouped, 512, POS)
@@ -391,7 +406,7 @@ def tile_guided_cam_module2_pa_kernel(
                 bn_relu(acc, m, cols)
             pool_bands(m, GPSIMD_BANDS, 12)
             if m == last_tile - 1:
-                neighbours_ends(0)
+                neighbours_ends(0, CO_TILES)
                 scale(0, CO_TILES, q_levels, True)
                 store(0)
                 k_levels = coarser_sums(CO_TILES, last_tile)
@@ -402,7 +417,8 @@ def tile_guided_cam_module2_pa_kernel(
             bn_relu(acc, last_tile, cols)
             if stop_band > first_band:
                 pool_bands(last_tile, first_band, stop_band)
+        neighbours_ends(CO_TILES, last_tile)
         scale(CO_TILES, last_tile, k_levels, True)
-        neighbours_ends(1)
+        neighbours_ends(last_tile, M_TILES)
         scale(last_tile, M_TILES, coarser_sums(last_tile, M_TILES), False)
         store(1)

@@ -84,7 +84,7 @@ def tile_guided_cam_module2_pa_kernel(
 
     with ExitStack() as stack:
         keep = stack.enter_context(tc.tile_pool(name="keep", bufs=1))
-        stage = stack.enter_context(tc.tile_pool(name="stage", bufs=5))
+        stage = stack.enter_context(tc.tile_pool(name="stage", bufs=4))
         halves = stack.enter_context(tc.tile_pool(name="halves", bufs=1))
         psum = stack.enter_context(tc.psum_pool(name="psum", bufs=8))
         stack.enter_context(tc.manual_schedule())
@@ -288,7 +288,7 @@ def tile_guided_cam_module2_pa_kernel(
             for level_sums, first, side in levels:
                 means = res[:, :, :, EDGE + first : EDGE + first + side * side]
                 means = means.rearrange("p b m f -> p m b f")
-                if on_scalar:
+                if on_scalar or side == GRID:
                     nc.scalar.mul(out=means, in_=level_sums, mul=float(side * side) / POS)
                 else:
                     nc.vector.tensor_scalar_mul(
@@ -340,8 +340,7 @@ def tile_guided_cam_module2_pa_kernel(
             if g == 3:
                 nc.vector.reciprocal(out=rstd[:], in_=rstd[:])
             quantise_cols(0, g, grouped, 0, 512)
-            if g < GROUPS - 1:
-                quantise_cols(0, g, grouped, 512, POS)
+            quantise_cols(0, g, grouped, 512, POS)
             for m in range(M_TILES):
                 mx_pass(first_accs[m], m, g, FIRST)
             if g == 2:
@@ -375,14 +374,14 @@ def tile_guided_cam_module2_pa_kernel(
         for m in range(emptied, M_TILES):
             bn_relu(first_accs[m], m, FIRST)
         regroup_cols(nc.vector.tensor_copy, 1, GROUPS - 1, grouped_1[GROUPS - 1], 0, 64)
-        for g in range(GROUPS):
+        for g in reversed(range(GROUPS)):
             quantise_cols(1, g, grouped_1[g], 0, 64)
-        quantise_cols(0, GROUPS - 1, grouped, 512, POS)
         two_rows = stage.tile(
             [P, CO_TILES, GPSIMD_BANDS, 2 * SIDE], F32, tag="grouped", align_bytes=64
         )
         pool_bands_gpsimd(VECTOR_FIRST_TILES, CO_TILES)
-        pool_bands_gpsimd(CO_TILES, M_TILES)
+        pool_bands_gpsimd(CO_TILES, M_TILES - 1)
+        pool_bands_gpsimd(M_TILES - 1, M_TILES)
         for m in range(VECTOR_FIRST_TILES):
             pool_bands(m, 0, GPSIMD_BANDS)
 
@@ -409,7 +408,6 @@ def tile_guided_cam_module2_pa_kernel(
                 neighbours_ends(0, CO_TILES)
                 scale(0, CO_TILES, q_levels, True)
                 store(0)
-                k_levels = coarser_sums(CO_TILES, last_tile)
         for cols, first_band, stop_band in ((MIDDLE, 0, 0), (LAST_A, GPSIMD_BANDS, 9), (LAST_B, 9, 12)):
             acc = new_acc(cols)
             for g in range(GROUPS):
@@ -418,7 +416,7 @@ def tile_guided_cam_module2_pa_kernel(
             if stop_band > first_band:
                 pool_bands(last_tile, first_band, stop_band)
         neighbours_ends(CO_TILES, last_tile)
-        scale(CO_TILES, last_tile, k_levels, True)
+        scale(CO_TILES, last_tile, coarser_sums(CO_TILES, last_tile), True)
         neighbours_ends(last_tile, M_TILES)
         scale(last_tile, M_TILES, coarser_sums(last_tile, M_TILES), False)
         store(1)

@@ -47,6 +47,8 @@ VECTOR_COLS = (384, 384)
 
 GPSIMD_BANDS = 4
 
+FIRST_BANDS = 5
+
 VECTOR_FIRST_TILES = 2
 
 BANKS_BEFORE_SLAB = (0, 2, 1, 1)
@@ -111,8 +113,11 @@ def tile_guided_cam_module2_pa_kernel(
         ]
         cell_sums = keep.tile([P, M_TILES, BANDS * GRID], F32, name="cell_sums")
 
-        one_row = halves.tile([P, CO_TILES, GPSIMD_BANDS, SIDE], F32, name="one_row")
-        two_cols = halves.tile([P, CO_TILES, GPSIMD_BANDS * GRID, 2], F32, name="two_cols")
+        one_row = halves.tile([P, CO_TILES * GPSIMD_BANDS * SIDE], F32, name="one_row")
+        two_cols = halves.tile([P, CO_TILES * GPSIMD_BANDS * GRID * 2], F32, name="two_cols")
+        q_first = halves.tile(
+            [P, CO_TILES - VECTOR_FIRST_TILES, FIRST_BANDS * GRID], F32, name="q_first"
+        )
 
         nc.vector.memset(w_planes[:].bitcast(I32), 0)
         warm_in = keep.tile([P, WARM_COLS], BF16, name="warm_in")
@@ -226,25 +231,30 @@ def tile_guided_cam_module2_pa_kernel(
                 op=ADD,
             )
 
-        def pool_bands_gpsimd(lo, hi):
-            rows = z[:, lo:hi, 0 : GPSIMD_BANDS * BAND].rearrange("p m (r h) -> p m r h", h=BAND)
+        def pool_bands_gpsimd(lo, hi, bands, sums):
             n = hi - lo
-            nc.gpsimd.tensor_add(
-                out=two_rows[:, 0:n], in0=rows[:, :, :, 0 : 2 * SIDE], in1=rows[:, :, :, 2 * SIDE : BAND]
+            rows = z[:, lo:hi, 0 : bands * BAND].rearrange("p m (r h) -> p m r h", h=BAND)
+            pairs = two_rows[:, 0 : n * bands * 2 * SIDE].rearrange(
+                "p (m r h) -> p m r h", r=bands, h=2 * SIDE
+            )
+            singles = one_row[:, 0 : n * bands * SIDE]
+            halves_of_cells = two_cols[:, 0 : n * bands * GRID * 2].rearrange(
+                "p (m f j) -> p m f j", m=n, j=2
             )
             nc.gpsimd.tensor_add(
-                out=one_row[:, 0:n],
-                in0=two_rows[:, 0:n, :, 0:SIDE],
-                in1=two_rows[:, 0:n, :, SIDE : 2 * SIDE],
-            )
-            cells = one_row[:, 0:n].rearrange("p m r (c j) -> p m (r c) j", j=CELL)
-            nc.gpsimd.tensor_add(
-                out=two_cols[:, 0:n], in0=cells[:, :, :, 0:2], in1=cells[:, :, :, 2:4]
+                out=pairs, in0=rows[:, :, :, 0 : 2 * SIDE], in1=rows[:, :, :, 2 * SIDE : BAND]
             )
             nc.gpsimd.tensor_add(
-                out=cell_sums[:, lo:hi, 0 : GPSIMD_BANDS * GRID],
-                in0=two_cols[:, 0:n, :, 0],
-                in1=two_cols[:, 0:n, :, 1],
+                out=singles.rearrange("p (m r h) -> p m r h", r=bands, h=SIDE),
+                in0=pairs[:, :, :, 0:SIDE],
+                in1=pairs[:, :, :, SIDE : 2 * SIDE],
+            )
+            cells = singles.rearrange("p (m f j) -> p m f j", m=n, j=CELL)
+            nc.gpsimd.tensor_add(
+                out=halves_of_cells, in0=cells[:, :, :, 0:2], in1=cells[:, :, :, 2:4]
+            )
+            nc.gpsimd.tensor_add(
+                out=sums, in0=halves_of_cells[:, :, :, 0], in1=halves_of_cells[:, :, :, 1]
             )
 
         def coarser_sums(lo, hi):
@@ -339,17 +349,18 @@ def tile_guided_cam_module2_pa_kernel(
             regroup_cols(nc.scalar.copy, 0, g, grouped, VECTOR_COLS[0], POS)
             if g == 3:
                 nc.vector.reciprocal(out=rstd[:], in_=rstd[:])
+                nc.vector.tensor_mul(out=slope[:], in0=gain, in1=rstd[:])
+                nc.vector.tensor_mul(out=shift[:], in0=shift[:], in1=rstd[:])
             quantise_cols(0, g, grouped, 0, 512)
             quantise_cols(0, g, grouped, 512, POS)
-            for m in range(M_TILES):
+            for m in range(M_TILES if g < GROUPS - 1 else CO_TILES):
                 mx_pass(first_accs[m], m, g, FIRST)
             if g == 2:
                 nc.vector.transpose(out=bn_cols[:], in_=bn_rows[:])
                 nc.vector.tensor_scalar_add(out=rstd[:], in0=var, scalar1=EPS)
                 nc.scalar.sqrt(out=rstd[:], in_=rstd[:])
                 nc.vector.tensor_mul(out=shift[:], in0=mean, in1=gain)
-        nc.vector.tensor_mul(out=shift[:], in0=shift[:], in1=rstd[:])
-        nc.vector.tensor_mul(out=slope[:], in0=gain, in1=rstd[:])
+        nc.vector.tensor_sub(out=shift[:], in0=bias, in1=shift[:])
         slope_m = slope[:].rearrange("p b c -> p (b c)")
         shift_m = shift[:].rearrange("p b c -> p (b c)")
 
@@ -360,8 +371,6 @@ def tile_guided_cam_module2_pa_kernel(
         for g in range(GROUPS):
             grouped_1.append(new_grouped())
             regroup_cols(nc.vector.tensor_copy, 1, g, grouped_1[g], POS - VECTOR_COLS[1], POS)
-            if g == 0:
-                nc.vector.tensor_sub(out=shift[:], in0=bias, in1=shift[:])
             for m in range(emptied, emptied + BANKS_BEFORE_SLAB[g]):
                 bn_relu(first_accs[m], m, FIRST)
             emptied += BANKS_BEFORE_SLAB[g]
@@ -369,21 +378,38 @@ def tile_guided_cam_module2_pa_kernel(
             if g > 0:
                 regroup_cols(nc.vector.tensor_copy, 1, g - 1, grouped_1[g - 1], 0, 64)
             quantise_cols(1, g, grouped_1[g], 64, POS)
-            for m in q_tiles:
-                mx_pass(last_accs[m], m, g, LAST)
+            if g == 0:
+                for m in (0, 1):
+                    mx_pass(last_accs[m], m, g, LAST)
+                    mx_pass(first_accs[CO_TILES + m], CO_TILES + m, GROUPS - 1, FIRST)
+                for m in (2, 3):
+                    mx_pass(first_accs[CO_TILES + m], CO_TILES + m, GROUPS - 1, FIRST)
+                mx_pass(last_accs[2], 2, g, LAST)
+            else:
+                for m in q_tiles:
+                    if g == 1 and m == 3:
+                        mx_pass(last_accs[m], m, 0, LAST)
+                    mx_pass(last_accs[m], m, g, LAST)
+            if g == GROUPS - 2:
+                early_acc = new_acc(LAST)
+                for early in (0, 1):
+                    mx_pass(early_acc, CO_TILES, early, LAST)
+        for early in (2, 3):
+            mx_pass(early_acc, CO_TILES, early, LAST)
         for m in range(emptied, M_TILES):
             bn_relu(first_accs[m], m, FIRST)
         regroup_cols(nc.vector.tensor_copy, 1, GROUPS - 1, grouped_1[GROUPS - 1], 0, 64)
         for g in reversed(range(GROUPS)):
             quantise_cols(1, g, grouped_1[g], 0, 64)
         two_rows = stage.tile(
-            [P, CO_TILES, GPSIMD_BANDS, 2 * SIDE], F32, tag="grouped", align_bytes=64
+            [P, CO_TILES * GPSIMD_BANDS * 2 * SIDE], F32, tag="grouped", align_bytes=64
         )
-        pool_bands_gpsimd(VECTOR_FIRST_TILES, CO_TILES)
-        pool_bands_gpsimd(CO_TILES, M_TILES - 1)
-        pool_bands_gpsimd(M_TILES - 1, M_TILES)
+        pool_bands_gpsimd(VECTOR_FIRST_TILES, CO_TILES, FIRST_BANDS, q_first[:])
+        pool_bands_gpsimd(
+            CO_TILES, M_TILES, GPSIMD_BANDS, cell_sums[:, CO_TILES:M_TILES, 0 : GPSIMD_BANDS * GRID]
+        )
         for m in range(VECTOR_FIRST_TILES):
-            pool_bands(m, 0, GPSIMD_BANDS)
+            pool_bands(m, 0, FIRST_BANDS)
 
         for m in q_tiles:
             bn_relu(last_accs[m], m, LAST)
@@ -393,15 +419,19 @@ def tile_guided_cam_module2_pa_kernel(
             for g in range(GROUPS):
                 mx_pass(acc, m, g, MIDDLE)
             bn_relu(acc, m, MIDDLE)
-            pool_bands(m, GPSIMD_BANDS, 7)
+            pool_bands(m, FIRST_BANDS, 7)
+        nc.scalar.copy(out=cell_sums[:, VECTOR_FIRST_TILES:CO_TILES, 0 : FIRST_BANDS * GRID], in_=q_first[:])
         q_levels = coarser_sums(0, CO_TILES)
 
         last_tile = M_TILES - 1
         for m in range(CO_TILES, last_tile):
             for cols in (LAST, MIDDLE):
-                acc = new_acc(cols)
-                for g in range(GROUPS):
-                    mx_pass(acc, m, g, cols)
+                if m == CO_TILES and cols == LAST:
+                    acc = early_acc
+                else:
+                    acc = new_acc(cols)
+                    for g in range(GROUPS):
+                        mx_pass(acc, m, g, cols)
                 bn_relu(acc, m, cols)
             pool_bands(m, GPSIMD_BANDS, 12)
             if m == last_tile - 1:

@@ -51,7 +51,7 @@ FIRST_BANDS = 5
 
 VECTOR_FIRST_TILES = 2
 
-BANKS_BEFORE_SLAB = (0, 2, 1, 1)
+BANKS_BEFORE_SLAB = (0, 1, 2, 1)
 
 WARM_MATMULS = 20
 WARM_COLS = 256
@@ -375,16 +375,14 @@ def tile_guided_cam_module2_pa_kernel(
                 bn_relu(first_accs[m], m, FIRST)
             emptied += BANKS_BEFORE_SLAB[g]
             regroup_cols(nc.scalar.copy, 1, g, grouped_1[g], 64, POS - VECTOR_COLS[1])
-            if g > 0:
-                regroup_cols(nc.vector.tensor_copy, 1, g - 1, grouped_1[g - 1], 0, 64)
+            small_copy = nc.scalar.copy if g == 0 else nc.vector.tensor_copy
+            regroup_cols(small_copy, 1, g, grouped_1[g], 0, 64)
             quantise_cols(1, g, grouped_1[g], 64, POS)
             if g == 0:
-                for m in (0, 1):
+                for m in range(3):
                     mx_pass(last_accs[m], m, g, LAST)
-                    mx_pass(first_accs[CO_TILES + m], CO_TILES + m, GROUPS - 1, FIRST)
-                for m in (2, 3):
-                    mx_pass(first_accs[CO_TILES + m], CO_TILES + m, GROUPS - 1, FIRST)
-                mx_pass(last_accs[2], 2, g, LAST)
+                    for k in range(CO_TILES + 2 * m, min(CO_TILES + 2 * m + 2, M_TILES)):
+                        mx_pass(first_accs[k], k, GROUPS - 1, FIRST)
             else:
                 for m in q_tiles:
                     if g == 1 and m == 3:
@@ -398,7 +396,6 @@ def tile_guided_cam_module2_pa_kernel(
             mx_pass(early_acc, CO_TILES, early, LAST)
         for m in range(emptied, M_TILES):
             bn_relu(first_accs[m], m, FIRST)
-        regroup_cols(nc.vector.tensor_copy, 1, GROUPS - 1, grouped_1[GROUPS - 1], 0, 64)
         for g in reversed(range(GROUPS)):
             quantise_cols(1, g, grouped_1[g], 0, 64)
         two_rows = stage.tile(

@@ -47,6 +47,8 @@ VECTOR_COLS = (384, 384)
 
 GPSIMD_BANDS = 4
 
+RUN = 2
+
 FIRST_BANDS = 5
 
 VECTOR_FIRST_TILES = 2
@@ -179,8 +181,8 @@ def tile_guided_cam_module2_pa_kernel(
 
         def regroup_cols(engine_copy, b, g, grouped, lo, hi):
             engine_copy(
-                out=grouped[:, lo:hi, :].rearrange("p (c i) t -> p c t i", i=4),
-                in_=raw[b][g][:, :, lo:hi].rearrange("p t (c i) -> p c t i", i=4),
+                out=grouped[:, lo:hi, :].rearrange("p (c i) t -> p c t i", i=RUN),
+                in_=raw[b][g][:, :, lo:hi].rearrange("p t (c i) -> p c t i", i=RUN),
             )
 
         def new_grouped():

@@ -327,11 +327,11 @@ def tile_guided_cam_module2_pa_kernel(
                 mul=float(GRID * GRID) / POS,
             )
 
-        def store(br):
+        def store(br, queues):
             rows = outs[br].rearrange("b (m i r) f -> i (b m) (r f)", i=P // GROUP, r=GROUP)
             done = 0
             for r, (first, count) in enumerate(CUTS):
-                nc.sync.dma_start(
+                queues[r % len(queues)].dma_start(
                     out=rows[:, :, done : done + count],
                     in_=rows_out[br][r:P:GROUP, :, :, first : first + count].rearrange(
                         "i b m f -> i (b m) f"
@@ -436,7 +436,7 @@ def tile_guided_cam_module2_pa_kernel(
             if m == last_tile - 1:
                 neighbours_ends(0, CO_TILES)
                 scale(0, CO_TILES, q_levels, True)
-                store(0)
+                store(0, (nc.sync,))
         for cols, first_band, stop_band in ((MIDDLE, 0, 0), (LAST_A, GPSIMD_BANDS, 9), (LAST_B, 9, 12)):
             acc = new_acc(cols)
             for g in range(GROUPS):
@@ -448,4 +448,4 @@ def tile_guided_cam_module2_pa_kernel(
         scale(CO_TILES, last_tile, coarser_sums(CO_TILES, last_tile), True)
         neighbours_ends(last_tile, M_TILES)
         scale(last_tile, M_TILES, coarser_sums(last_tile, M_TILES), False)
-        store(1)
+        store(1, (nc.sync, nc.scalar))

from contextlib import ExitStack

import concourse.mybir as mybir
from concourse.masks import make_identity

BF16 = mybir.dt.bfloat16
F32 = mybir.dt.float32
I32 = mybir.dt.int32
U32 = mybir.dt.uint32
U8 = mybir.dt.uint8
FP8X4 = mybir.dt.float8_e4m3fn_x4
ADD = mybir.AluOpType.add
RELU = mybir.ActivationFunctionType.Relu

P = 128
PACK = 4
K_PASS = P * PACK
BATCH = 2
CHANNELS = 2048
GROUPS = CHANNELS // K_PASS
CO = 512
BRANCHES = 2
CO_TILES = CO // P
M_TILES = BRANCHES * CO_TILES
SIDE = 24
POS = SIDE * SIDE
COLS = BATCH * POS
CELL = 4
GRID = SIDE // CELL
BAND = CELL * SIDE
BANDS = COLS // BAND
EPS = 1e-5
FEATS = 50

GROUP = 4
EDGE = 6
ROW = EDGE + FEATS
CUTS = ((EDGE, 48), (EDGE - 2, 48), (EDGE - 4, 48), (0, ROW))

FIRST = (0, 512)
MIDDLE = (512, 640)
LAST = (640, 1152)
LAST_A = (640, 896)
LAST_B = (896, 1152)

VECTOR_COLS = (384, 384)

GPSIMD_BANDS = 4

RUN = 2

FIRST_BANDS = 5

VECTOR_FIRST_TILES = 2

BANKS_BEFORE_SLAB = (0, 1, 2, 1)

WARM_MATMULS = 20
WARM_COLS = 256

FLOPS = 2 * BRANCHES * BATCH * CO * CHANNELS * POS


def tile_guided_cam_module2_pa_kernel(
    tc,
    x,
    wq_words,
    wq_scales,
    q_scale,
    q_bias,
    q_mean,
    q_var,
    wk_words,
    wk_scales,
    k_scale,
    k_bias,
    k_mean,
    k_var,
    out_0,
    out_1,
):
    nc = tc.nc
    words_in = (wq_words, wk_words)
    scales_in = (wq_scales, wk_scales)
    bn_in = (q_scale, q_bias, q_mean, q_var, k_scale, k_bias, k_mean, k_var)
    outs = (out_0, out_1)
    x_rows = x.rearrange("b c h w -> b c (h w)")

    with ExitStack() as stack:
        keep = stack.enter_context(tc.tile_pool(name="keep", bufs=1))
        stage = stack.enter_context(tc.tile_pool(name="stage", bufs=4))
        halves = stack.enter_context(tc.tile_pool(name="halves", bufs=1))
        psum = stack.enter_context(tc.psum_pool(name="psum", bufs=8))
        stack.enter_context(tc.manual_schedule())

        raw = [
            [keep.tile([P, PACK, POS], BF16, name="raw%d%d" % (b, g)) for g in range(GROUPS)]
            for b in range(BATCH)
        ]
        w_words = [
            keep.tile([P, GROUPS, CO], U32, name="w_words%d" % br, align_bytes=64)
            for br in range(BRANCHES)
        ]
        w_planes = keep.tile([P, BRANCHES, CO], U8, name="w_planes", align_bytes=64)
        x_words = keep.tile([P, GROUPS, COLS], U32, name="x_words", align_bytes=64)
        x_planes = keep.tile([P, GROUPS, COLS], U8, name="x_planes", align_bytes=64)
        bn_rows = keep.tile([P, 32], BF16, name="bn_rows", align_bytes=64)
        bn_cols = keep.tile([P, 32], BF16, name="bn_cols", align_bytes=64)
        warm = keep.tile([P, 1], F32, name="warm")
        z = keep.tile([P, M_TILES, COLS], F32, name="z")
        down_one = keep.tile([P, P + 1], F32, name="down_one")
        rows_out = [
            keep.tile([P, BATCH, CO_TILES, ROW], F32, name="rows_out%d" % br, align_bytes=64)
            for br in range(BRANCHES)
        ]
        cell_sums = keep.tile([P, M_TILES, BANDS * GRID], F32, name="cell_sums")

        one_row = halves.tile([P, CO_TILES * GPSIMD_BANDS * SIDE], F32, name="one_row")
        two_cols = halves.tile([P, CO_TILES * GPSIMD_BANDS * GRID * 2], F32, name="two_cols")
        q_first = halves.tile(
            [P, CO_TILES - VECTOR_FIRST_TILES, FIRST_BANDS * GRID], F32, name="q_first"
        )

        nc.vector.memset(w_planes[:].bitcast(I32), 0)
        warm_in = keep.tile([P, WARM_COLS], BF16, name="warm_in")
        nc.vector.memset(warm_in[:], 0.0)
        warm_acc = psum.tile([P, 512], F32, tag="acc", name="warm_acc")
        for i in range(WARM_MATMULS):
            nc.tensor.matmul(
                out=warm_acc[:, 0:WARM_COLS], lhsT=warm_in[:, 0:P], rhs=warm_in[:], start=True, stop=True
            )
        nc.vector.memset(warm[:], 1.0)
        nc.scalar.sqrt(out=warm[:], in_=warm[:])

        def load_x(b, g):
            rows = x_rows[b, g * K_PASS : (g + 1) * K_PASS, :]
            nc.sync.dma_start(out=raw[b][g][:], in_=rows.rearrange("(p t) n -> p t n", t=PACK))

        def load_words(br, g):
            nc.sync.dma_start(
                out=w_words[br][:, g, :].bitcast(I32),
                in_=words_in[br][g].rearrange("p n t -> p (n t)").bitcast(I32),
            )

        def load_planes(br):
            for quad in range(4):
                nc.sync.dma_start(
                    out=w_planes[32 * quad : 32 * quad + 16, br, :].bitcast(I32),
                    in_=scales_in[br][:, 4 * quad : 4 * quad + 4, :].bitcast(I32),
                )

        def load_bn(br, queue):
            for v in range(4 * br, 4 * br + 4):
                queue.dma_start(
                    out=bn_rows[v : P : len(bn_in), :],
                    in_=bn_in[v].rearrange("(c q i) -> q c i", c=CO_TILES, i=32),
                )

        load_bn(1, nc.gpsimd)
        nc.gpsimd.memset(down_one[:, 0:1], 0.0)
        make_identity(nc, down_one[:, 1 : P + 1])
        load_x(0, 0)
        load_planes(0)
        load_words(0, 0)
        load_x(0, 1)
        load_words(1, 0)
        load_planes(1)
        load_x(0, 2)
        load_words(0, 1)
        load_words(1, 1)
        load_bn(0, nc.sync)
        load_x(0, 3)
        load_words(0, 2)
        load_words(1, 2)
        load_x(1, 0)
        load_words(0, 3)
        load_x(1, 1)
        load_words(1, 3)
        load_x(1, 2)
        load_x(1, 3)

        def regroup_cols(engine_copy, b, g, grouped, lo, hi):
            engine_copy(
                out=grouped[:, lo:hi, :].rearrange("p (c i) t -> p c t i", i=RUN),
                in_=raw[b][g][:, :, lo:hi].rearrange("p t (c i) -> p c t i", i=RUN),
            )

        def new_grouped():
            return stage.tile([P, POS, PACK], BF16, tag="grouped", align_bytes=64, name="grouped")

        def quantise_cols(b, g, grouped, lo, hi):
            nc.vector.quantize_mx(
                out=x_words[:, g, b * POS + lo : b * POS + hi].bitcast(FP8X4),
                scales=x_planes[:, g, b * POS + lo : b * POS + hi],
                in_=grouped[:, lo:hi, :].rearrange("p n t -> p (n t)"),
            )

        def mx_pass(acc, m, g, cols):
            br, co = divmod(m, CO_TILES)
            co_cols = slice(co * P, (co + 1) * P)
            nc.tensor.matmul_mx(
                out=acc,
                lhsT=w_words[br][:, g, co_cols].bitcast(FP8X4),
                lhsT_scale=w_planes[4 * g : P, br, co_cols],
                rhs=x_words[:, g, cols[0] : cols[1]].bitcast(FP8X4),
                rhs_scale=x_planes[:, g, cols[0] : cols[1]],
                start=(g == 0),
                stop=(g == GROUPS - 1),
            )

        def new_acc(cols):
            acc = psum.tile([P, 512], F32, tag="acc")
            return acc[:, 0 : cols[1] - cols[0]]

        def bn_relu(acc, m, cols):
            nc.scalar.activation(
                out=z[:, m, cols[0] : cols[1]],
                in_=acc,
                func=RELU,
                bias=shift_m[:, m : m + 1],
                scale=slope_m[:, m : m + 1],
            )

        def pool_bands(m, first, stop):
            nc.vector.tensor_reduce(
                out=cell_sums[:, m, first * GRID : stop * GRID].rearrange(
                    "p (r c) -> p r c", c=GRID
                ),
                in_=z[:, m, first * BAND : stop * BAND].rearrange(
                    "p (r i c j) -> p r c i j", i=CELL, c=GRID, j=CELL
                ),
                axis=mybir.AxisListType.XY,
                op=ADD,
            )

        def pool_bands_gpsimd(lo, hi, bands, sums):
            n = hi - lo
            rows = z[:, lo:hi, 0 : bands * BAND].rearrange("p m (r h) -> p m r h", h=BAND)
            pairs = two_rows[:, 0 : n * bands * 2 * SIDE].rearrange(
                "p (m r h) -> p m r h", r=bands, h=2 * SIDE
            )
            singles = one_row[:, 0 : n * bands * SIDE]
            halves_of_cells = two_cols[:, 0 : n * bands * GRID * 2].rearrange(
                "p (m f j) -> p m f j", m=n, j=2
            )
            nc.gpsimd.tensor_add(
                out=pairs, in0=rows[:, :, :, 0 : 2 * SIDE], in1=rows[:, :, :, 2 * SIDE : BAND]
            )
            nc.gpsimd.tensor_add(
                out=singles.rearrange("p (m r h) -> p m r h", r=bands, h=SIDE),
                in0=pairs[:, :, :, 0:SIDE],
                in1=pairs[:, :, :, SIDE : 2 * SIDE],
            )
            cells = singles.rearrange("p (m f j) -> p m f j", m=n, j=CELL)
            nc.gpsimd.tensor_add(
                out=halves_of_cells, in0=cells[:, :, :, 0:2], in1=cells[:, :, :, 2:4]
            )
            nc.gpsimd.tensor_add(
                out=sums, in0=halves_of_cells[:, :, :, 0], in1=halves_of_cells[:, :, :, 1]
            )

        def coarser_sums(lo, hi):
            n = hi - lo
            sums = cell_sums[:, lo:hi, :]
            sums3 = keep.tile([P, n, BATCH, 9], F32, name="sums3_%d" % lo)
            sums2 = keep.tile([P, n, BATCH, 4], F32, name="sums2_%d" % lo)
            sums1 = keep.tile([P, n, BATCH, 1], F32, name="sums1_%d" % lo)
            nc.vector.tensor_reduce(
                out=sums2[:].rearrange("p m b (r c) -> p (m b r) c", c=2),
                in_=sums.rearrange("p m (b r i c j) -> p (m b r) c i j", b=BATCH, r=2, i=3, c=2, j=3),
                axis=mybir.AxisListType.XY,
                op=ADD,
            )
            nc.vector.tensor_reduce(
                out=sums3[:].rearrange("p m b (r c) -> p (m b r) c", c=3),
                in_=sums.rearrange("p m (b r i c j) -> p (m b r) c i j", b=BATCH, r=3, i=2, c=3, j=2),
                axis=mybir.AxisListType.XY,
                op=ADD,
            )
            nc.vector.tensor_reduce(
                out=sums1[:].rearrange("p m b o -> p (m b) o"),
                in_=(
                    sums2[:].rearrange("p m b f -> p (m b) f")
                    if n > 1
                    else sums.rearrange("p m (b f) -> p (m b) f", b=BATCH)
                ),
                axis=mybir.AxisListType.X,
                op=ADD,
            )
            return (
                (sums.rearrange("p m (b f) -> p m b f", b=BATCH), 14, 6),
                (sums2[:], 1, 2),
                (sums3[:], 5, 3),
                (sums1[:], 0, 1),
            )

        def scale(lo, hi, levels, on_scalar):
            br, first_tile = divmod(lo, CO_TILES)
            res = rows_out[br][:, :, first_tile : first_tile + hi - lo, :]
            for level_sums, first, side in levels:
                means = res[:, :, :, EDGE + first : EDGE + first + side * side]
                means = means.rearrange("p b m f -> p m b f")
                if on_scalar or side == GRID:
                    nc.scalar.mul(out=means, in_=level_sums, mul=float(side * side) / POS)
                else:
                    nc.vector.tensor_scalar_mul(
                        out=means, in0=level_sums, scalar1=float(side * side) / POS
                    )

        def neighbours_ends(lo, hi):
            br, first_tile = divmod(lo, CO_TILES)
            n = (hi - lo) * BATCH
            res = rows_out[br][:, :, first_tile : first_tile + hi - lo, 0:EDGE]
            acc = psum.tile([P, 512], F32, tag="acc")
            nc.tensor.matmul(
                out=acc[:, 0 : n * EDGE].rearrange("p (k f) -> p k f", f=EDGE),
                lhsT=down_one[:, 0:P],
                rhs=cell_sums[:, lo:hi, :].rearrange("p m (b f) -> p (m b) f", b=BATCH)[
                    :, :, GRID * (GRID - 1) : GRID * GRID
                ],
                start=True,
                stop=True,
            )
            nc.scalar.mul(
                out=res.rearrange("p b m f -> p m b f"),
                in_=acc[:, 0 : n * EDGE].rearrange("p (m b f) -> p m b f", b=BATCH, f=EDGE),
                mul=float(GRID * GRID) / POS,
            )

        def store(br, queues):
            rows = outs[br].rearrange("b (m i r) f -> i (b m) (r f)", i=P // GROUP, r=GROUP)
            done = 0
            for r, (first, count) in enumerate(CUTS):
                queues[r % len(queues)].dma_start(
                    out=rows[:, :, done : done + count],
                    in_=rows_out[br][r:P:GROUP, :, :, first : first + count].rearrange(
                        "i b m f -> i (b m) f"
                    ),
                )
                done += count

        by_kind = bn_cols[:].rearrange("p (c b k) -> p b k c", b=BRANCHES, k=4)
        gain, bias, mean, var = [by_kind[:, :, kind, :] for kind in range(4)]
        rstd = keep.tile([P, BRANCHES, CO_TILES], F32, name="rstd")
        slope = keep.tile([P, BRANCHES, CO_TILES], F32, name="slope")
        shift = keep.tile([P, BRANCHES, CO_TILES], F32, name="shift")
        first_accs = [new_acc(FIRST) for m in range(M_TILES)]
        for g in range(GROUPS):
            grouped = new_grouped()
            regroup_cols(nc.vector.tensor_copy, 0, g, grouped, 0, VECTOR_COLS[0])
            regroup_cols(nc.scalar.copy, 0, g, grouped, VECTOR_COLS[0], POS)
            if g == 3:
                nc.vector.reciprocal(out=rstd[:], in_=rstd[:])
                nc.vector.tensor_mul(out=slope[:], in0=gain, in1=rstd[:])
                nc.vector.tensor_mul(out=shift[:], in0=shift[:], in1=rstd[:])
            quantise_cols(0, g, grouped, 0, 512)
            quantise_cols(0, g, grouped, 512, POS)
            for m in range(M_TILES if g < GROUPS - 1 else CO_TILES):
                mx_pass(first_accs[m], m, g, FIRST)
            if g == 2:
                nc.vector.transpose(out=bn_cols[:], in_=bn_rows[:])
                nc.vector.tensor_scalar_add(out=rstd[:], in0=var, scalar1=EPS)
                nc.scalar.sqrt(out=rstd[:], in_=rstd[:])
                nc.vector.tensor_mul(out=shift[:], in0=mean, in1=gain)
        nc.vector.tensor_sub(out=shift[:], in0=bias, in1=shift[:])
        slope_m = slope[:].rearrange("p b c -> p (b c)")
        shift_m = shift[:].rearrange("p b c -> p (b c)")

        q_tiles = range(CO_TILES)
        last_accs = [new_acc(LAST) for m in q_tiles]
        grouped_1 = []
        emptied = 0
        for g in range(GROUPS):
            grouped_1.append(new_grouped())
            regroup_cols(nc.vector.tensor_copy, 1, g, grouped_1[g], POS - VECTOR_COLS[1], POS)
            for m in range(emptied, emptied + BANKS_BEFORE_SLAB[g]):
                bn_relu(first_accs[m], m, FIRST)
            emptied += BANKS_BEFORE_SLAB[g]
            regroup_cols(nc.scalar.copy, 1, g, grouped_1[g], 64, POS - VECTOR_COLS[1])
            small_copy = nc.scalar.copy if g == 0 else nc.vector.tensor_copy
            regroup_cols(small_copy, 1, g, grouped_1[g], 0, 64)
            quantise_cols(1, g, grouped_1[g], 64, POS)
            if g == 0:
                for m in range(3):
                    mx_pass(last_accs[m], m, g, LAST)
                    for k in range(CO_TILES + 2 * m, min(CO_TILES + 2 * m + 2, M_TILES)):
                        mx_pass(first_accs[k], k, GROUPS - 1, FIRST)
            else:
                for m in q_tiles:
                    if g == 1 and m == 3:
                        mx_pass(last_accs[m], m, 0, LAST)
                    mx_pass(last_accs[m], m, g, LAST)
            if g == GROUPS - 2:
                early_acc = new_acc(LAST)
                for early in (0, 1):
                    mx_pass(early_acc, CO_TILES, early, LAST)
        for early in (2, 3):
            mx_pass(early_acc, CO_TILES, early, LAST)
        for m in range(emptied, M_TILES):
            bn_relu(first_accs[m], m, FIRST)
        for g in reversed(range(GROUPS)):
            quantise_cols(1, g, grouped_1[g], 0, 64)
        two_rows = stage.tile(
            [P, CO_TILES * GPSIMD_BANDS * 2 * SIDE], F32, tag="grouped", align_bytes=64
        )
        pool_bands_gpsimd(VECTOR_FIRST_TILES, CO_TILES, FIRST_BANDS, q_first[:])
        pool_bands_gpsimd(
            CO_TILES, M_TILES, GPSIMD_BANDS, cell_sums[:, CO_TILES:M_TILES, 0 : GPSIMD_BANDS * GRID]
        )
        for m in range(VECTOR_FIRST_TILES):
            pool_bands(m, 0, FIRST_BANDS)

        for m in q_tiles:
            bn_relu(last_accs[m], m, LAST)
            pool_bands(m, 7, 12)
        for m in q_tiles:
            acc = new_acc(MIDDLE)
            for g in range(GROUPS):
                mx_pass(acc, m, g, MIDDLE)
            bn_relu(acc, m, MIDDLE)
            pool_bands(m, FIRST_BANDS, 7)
        nc.scalar.copy(out=cell_sums[:, VECTOR_FIRST_TILES:CO_TILES, 0 : FIRST_BANDS * GRID], in_=q_first[:])
        q_levels = coarser_sums(0, CO_TILES)

        last_tile = M_TILES - 1
        for m in range(CO_TILES, last_tile):
            for cols in (LAST, MIDDLE):
                if m == CO_TILES and cols == LAST:
                    acc = early_acc
                else:
                    acc = new_acc(cols)
                    for g in range(GROUPS):
                        mx_pass(acc, m, g, cols)
                bn_relu(acc, m, cols)
            pool_bands(m, GPSIMD_BANDS, 12)
            if m == last_tile - 1:
                neighbours_ends(0, CO_TILES)
                scale(0, CO_TILES, q_levels, True)
                store(0, (nc.sync,))
        for cols, first_band, stop_band in ((MIDDLE, 0, 0), (LAST_A, GPSIMD_BANDS, 9), (LAST_B, 9, 12)):
            acc = new_acc(cols)
            for g in range(GROUPS):
                mx_pass(acc, last_tile, g, cols)
            bn_relu(acc, last_tile, cols)
            if stop_band > first_band:
                pool_bands(last_tile, first_band, stop_band)
        neighbours_ends(CO_TILES, last_tile)
        scale(CO_TILES, last_tile, coarser_sums(CO_TILES, last_tile), True)
        neighbours_ends(last_tile, M_TILES)
        scale(last_tile, M_TILES, coarser_sums(last_tile, M_TILES), False)
        store(1, (nc.sync, nc.scalar))
